import numpy as np
import ml_dtypes


def mxq(x, axis, fmt="e4m3"):
    dtype, down = {"e4m3": (ml_dtypes.float8_e4m3fn, 7), "e5m2": (ml_dtypes.float8_e5m2, 14)}[fmt]
    v = np.moveaxis(np.asarray(x, np.float32).astype(ml_dtypes.bfloat16).astype(np.float64), axis, -1)
    blocks = v.reshape(v.shape[:-1] + (-1, 32))
    amax = np.abs(blocks).max(-1, keepdims=True)
    byte = np.maximum(np.where(amax > 0, np.frexp(amax)[1] - 1 + 127, 0) - down, 1)
    scale = np.exp2(byte - 127.0)
    codes = (blocks / scale).astype(np.float32).astype(dtype).astype(np.float64)
    return np.moveaxis((codes * scale).reshape(v.shape), -1, axis)


WIDE = False


def mx_kscale(k):
    if not WIDE:
        return np.ones(k)
    levels = np.array([10, -10, 5, -5, 0])
    a = np.random.permutation(np.resize(levels, k // 512 * 4)).reshape(k // 512, 4)
    idx = np.arange(k)
    return np.exp2(a[idx // 512, idx % 128 // 32])


BF16 = ml_dtypes.bfloat16


def bf(x):
    return np.asarray(x, np.float32).astype(BF16)


def f64(x):
    return np.asarray(x).astype(np.float64)


E2M1 = np.array([0.0, 0.5, 1.0, 1.5, 2.0, 3.0, 4.0, 6.0, -0.0, -0.5, -1.0, -1.5, -2.0, -3.0, -4.0, -6.0])


def pack_weight(w, fmt):
    k, n = w.shape
    w = f64(bf(w)).reshape(k // 32, 32, n)
    amax = np.abs(w).max(1)
    if fmt == "e4m3":
        byte = np.frexp(amax)[1] - 1 + 127 - 7
    else:
        mant, ex = np.frexp(amax / 6.0)
        byte = np.where(mant > 0.5, ex, ex - 1) + 127
    byte = np.clip(np.where(amax > 0, byte, 1), 1, 254)
    scaled = (w * np.exp2(127.0 - byte)[:, None, :]).reshape(k, n).astype(np.float32)
    by_word = np.ascontiguousarray(scaled.reshape(k // 512, 128, 4, n).transpose(0, 1, 3, 2))
    if fmt == "e4m3":
        words = by_word.astype(ml_dtypes.float8_e4m3fn).view(np.uint8)
    else:
        c = by_word.astype(ml_dtypes.float4_e2m1fn).view(np.uint8) & 0xF
        words = c[..., 0::2] | (c[..., 1::2] << 4)
    return np.ascontiguousarray(words), np.ascontiguousarray(byte.astype(np.uint8).reshape(k // 512, 16, n))


def unpack_weight(words, scales, fmt):
    g, p, n, _ = words.shape
    if fmt == "e4m3":
        vals = np.ascontiguousarray(words).view(ml_dtypes.float8_e4m3fn).astype(np.float64)
    else:
        nib = np.empty((g, p, n, 4), np.uint8)
        nib[..., 0::2] = words & 0xF
        nib[..., 1::2] = words >> 4
        vals = E2M1[nib]
    vals = vals * np.repeat(np.exp2(scales.astype(np.float64) - 127.0), 8, axis=1)[..., None]
    return vals.transpose(0, 1, 3, 2).reshape(g * 512, n)

def pack4(w):
    words, scales = pack_weight(w, "e2m1")
    return words.reshape(words.shape[0], 128, -1), scales


def unpack4(words, scales):
    return unpack_weight(words.reshape(words.shape[0], 128, -1, 2), scales, "e2m1")


B, IN_CH, OUT_CH, KH, KW, H, W_IN = 4, 16, 256, 4, 4, 35, 35
HO, WO = H - KH + 1, W_IN - KW + 1
L = HO * WO
KD = KH * KW
F = IN_CH * KD * KD
MXB = 32


def setup_inputs():
    s = mx_kscale(F)[(np.arange(IN_CH) * KD * KD) // MXB * MXB]
    u = np.exp2(np.round(np.log2(s) / 2))
    x = bf(np.random.standard_normal((B, IN_CH, H, W_IN)) * u[None, :, None, None])
    w = np.random.standard_normal((OUT_CH, F)) / np.sqrt(F) / np.repeat(u * u, KD * KD)[None, :]
    words, scales = pack4(np.ascontiguousarray(w.T))
    return {"x": x, "W_words": words, "W_scales": scales}


def _unfold(x):
    patches = np.stack([x[:, :, i:i + HO, j:j + WO] for i in range(KH) for j in range(KW)], axis=2)
    return patches.reshape(B, IN_CH, KD, L).transpose(0, 3, 1, 2)


def reference(x, W_words, W_scales):
    p = _unfold(f64(x))
    outer = np.einsum("blci,blcj->blcij", p, p)
    feat = outer.reshape(B, L, F)
    out = unpack4(W_words, W_scales).T @ mxq(feat, 2, "e4m3").transpose(0, 2, 1)
    return out.reshape(B, OUT_CH, HO, WO)

@@ -1,0 +1,175 @@
+from contextlib import ExitStack
+
+import concourse.mybir as mybir
+
+BF16 = mybir.dt.bfloat16
+F32 = mybir.dt.float32
+I32 = mybir.dt.int32
+U8 = mybir.dt.uint8
+U32 = mybir.dt.uint32
+FP8X4 = mybir.dt.float8_e4m3fn_x4
+FP4X4 = mybir.dt.float4_e2m1fn_x4
+
+P = 128
+PACK = 4
+IMAGES = 4
+CHANNELS = 16
+SIDE = 35
+PIXELS = SIDE * SIDE
+GRID = 32
+QUADS = GRID // PACK
+PHASES = PACK
+PASSES = 8
+SHIFTS = PHASES + 2
+TILE_ROWS = 16
+N_TILE = TILE_ROWS * GRID
+TILES_PER_IMAGE = GRID // TILE_ROWS
+OUT_CH = 256
+M_TILES = OUT_CH // P
+HELD_ROW = QUADS * PACK
+FLOPS = 2 * IMAGES * GRID * GRID * CHANNELS * 256 * OUT_CH
+
+
+def tile_fast2order_de_conv_kernel(tc, x, W_words, W_scales, out):
+    nc = tc.nc
+    with ExitStack() as ctx:
+        keep = ctx.enter_context(tc.tile_pool(name="keep", bufs=1))
+        feats = ctx.enter_context(tc.tile_pool(name="feats", bufs=3))
+        packed = ctx.enter_context(tc.tile_pool(name="packed", bufs=4))
+        results = ctx.enter_context(tc.tile_pool(name="results", bufs=4))
+        psum = ctx.enter_context(tc.psum_pool(name="psum", bufs=4))
+
+        w_planes = keep.tile([P, PASSES, OUT_CH], U8, align_bytes=64)
+        nc.vector.memset(w_planes[:].bitcast(I32), 0)
+
+        x_flat = x.rearrange("n c h w -> n c (h w)")
+        x_held = []
+        x_window = []
+
+        def load_image(n):
+            x_held.append(keep.tile([P, PIXELS], BF16, name="x_held%d" % n))
+            x_window.append(keep.tile([P, GRID * SIDE], BF16, name="x_window%d" % n))
+            for jh in range(4):
+                rows = x_flat[n, :, SIDE * jh : SIDE * jh + GRID * SIDE]
+                nc.scalar.dma_start(
+                    out=x_window[n][jh:P:4, :],
+                    in_=rows.unsqueeze(1).to_broadcast([CHANNELS, 2, GRID * SIDE]),
+                )
+            for iw0 in range(2):
+                for jh in range(4):
+                    nc.sync.dma_start(
+                        out=x_held[n][4 * iw0 + jh : P : 8, 0 : PIXELS - 1],
+                        in_=x_flat[n, :, iw0 : iw0 + PIXELS - 1],
+                    )
+
+        load_image(0)
+
+        scale_rows = W_scales.rearrange("g (c2 a) o -> (g c2) (a o)", c2=2)
+        for quadrant in range(4):
+            nc.sync.dma_start(
+                out=w_planes[32 * quadrant : 32 * quadrant + 4].rearrange("p a o -> p (a o)").bitcast(I32),
+                in_=scale_rows[4 * quadrant : 4 * quadrant + 4, :].bitcast(I32),
+            )
+
+        w_words = keep.tile([P, PASSES, 2 * OUT_CH], U8, align_bytes=64)
+        words_by_pass = W_words.rearrange("g (c2 a r) b -> a (g c2) r b", c2=2, a=PASSES)
+        for a in range(PASSES):
+            nc.sync.dma_start(out=w_words[:, a, :].bitcast(I32), in_=words_by_pass[a].bitcast(I32))
+
+        for n in range(1, IMAGES):
+            load_image(n)
+
+        held = []
+        windows = []
+
+        def table_pieces(n):
+            held.append(keep.tile([P, SHIFTS, SIDE * HELD_ROW], BF16, name="held%d" % n))
+            windows.append(keep.tile([P, PHASES, GRID * GRID], BF16, name="windows%d" % n))
+            window_rows = x_window[n][:].rearrange("p (y w) -> p y w", w=SIDE)
+            held_rows = x_held[n][:].rearrange("p (h w) -> p h w", w=SIDE)
+            pieces = []
+            for phase in range(PHASES):
+                pieces.append(
+                    (
+                        windows[n][:, phase, :].rearrange("p (y u) -> p y u", u=GRID),
+                        window_rows[:, :, phase : phase + GRID],
+                    )
+                )
+            for shift in range(SHIFTS):
+                every_fourth = held_rows[:, :, shift : shift + PACK * (QUADS - 1) + 1 : PACK]
+                pieces.append(
+                    (
+                        held[n][:, shift, :].rearrange("p (h q t) -> p h q t", q=QUADS, t=PACK),
+                        every_fourth.unsqueeze(3).to_broadcast([P, SIDE, QUADS, PACK]),
+                    )
+                )
+            return pieces
+
+        first_pieces = table_pieces(0)
+        for destination, source in first_pieces[: PHASES + PHASES]:
+            nc.vector.tensor_copy(out=destination, in_=source)
+        for destination, source in first_pieces[PHASES + PHASES :]:
+            nc.scalar.copy(out=destination, in_=source)
+
+        steps = [(n, half, a) for n in range(IMAGES) for half in range(TILES_PER_IMAGE) for a in range(PASSES)]
+
+        def multiply(n, half, a):
+            ih, iwh = a // 2, a % 2
+            first_row = TILE_ROWS * half + ih
+            feat = feats.tile([P, PHASES, PACK * N_TILE // PHASES], BF16, name="feat", align_bytes=64)
+            nc.vector.tensor_tensor(
+                out=feat[:],
+                in0=held[n][:, 2 * iwh : 2 * iwh + PHASES, HELD_ROW * first_row : HELD_ROW * (first_row + TILE_ROWS)],
+                in1=windows[n][:, :, GRID * TILE_ROWS * half : GRID * TILE_ROWS * (half + 1)],
+                op=mybir.AluOpType.mult,
+            )
+            return feat
+
+        sums = []
+        later_pieces = []
+        feat_next = multiply(*steps[0])
+        for k, (n, half, a) in enumerate(steps):
+            feat = feat_next
+            if k + 1 < len(steps):
+                feat_next = multiply(*steps[k + 1])
+            codes = packed.tile([P, N_TILE], U32, name="codes", align_bytes=64)
+            scales = packed.tile([P, N_TILE], U8, name="scales", align_bytes=64)
+            nc.vector.quantize_mx(
+                out=codes[:].bitcast(FP8X4),
+                scales=scales[:],
+                in_=feat[:].rearrange("p s e -> p (s e)"),
+            )
+
+            if a == 0:
+                sums = [psum.tile([P, N_TILE], F32, name="sums%d" % m) for m in range(M_TILES)]
+            for m in range(M_TILES):
+                nc.tensor.matmul_mx(
+                    out=sums[m][:],
+                    lhsT=w_words[:, a, 2 * P * m : 2 * P * (m + 1)].bitcast(FP4X4),
+                    lhsT_scale=w_planes[:, a, P * m : P * (m + 1)],
+                    rhs=codes[:].bitcast(FP8X4),
+                    rhs_scale=scales[:],
+                    start=(a == 0),
+                    stop=(a == PASSES - 1),
+                )
+
+            if half == 0 and a == 0:
+                later_pieces = table_pieces(n + 1) if n + 1 < IMAGES else []
+            step_in_image = PASSES * half + a
+            if step_in_image < len(later_pieces):
+                destination, source = later_pieces[step_in_image]
+                nc.scalar.copy(out=destination, in_=source)
+
+            if a == PASSES - 1:
+                for m in range(M_TILES):
+                    result = results.tile([P, TILE_ROWS, QUADS, PHASES], F32, name="result")
+                    nc.scalar.copy(
+                        out=result[:],
+                        in_=sums[m][:].rearrange("o (s y q) -> o y q s", s=PHASES, y=TILE_ROWS),
+                    )
+                    nc.sync.dma_start(
+                        out=out[n, P * m : P * (m + 1), TILE_ROWS * half : TILE_ROWS * (half + 1), :].rearrange(
+                            "o y z -> o (y z)"
+                        ),
+                        in_=result[:].rearrange("o y q s -> o (y q s)"),
+                    )

@@ -27,17 +27,19 @@ TILES_PER_IMAGE = GRID // TILE_ROWS
 OUT_CH = 256
 M_TILES = OUT_CH // P
 HELD_ROW = QUADS * PACK
+PIECES_PER_STEP = 2
 FLOPS = 2 * IMAGES * GRID * GRID * CHANNELS * 256 * OUT_CH
 
 
 def tile_fast2order_de_conv_kernel(tc, x, W_words, W_scales, out):
     nc = tc.nc
     with ExitStack() as ctx:
+        ctx.enter_context(tc.manual_schedule())
         keep = ctx.enter_context(tc.tile_pool(name="keep", bufs=1))
         feats = ctx.enter_context(tc.tile_pool(name="feats", bufs=3))
         packed = ctx.enter_context(tc.tile_pool(name="packed", bufs=4))
         results = ctx.enter_context(tc.tile_pool(name="results", bufs=4))
-        psum = ctx.enter_context(tc.psum_pool(name="psum", bufs=4))
+        psum = ctx.enter_context(tc.psum_pool(name="psum", bufs=2))
 
         w_planes = keep.tile([P, PASSES, OUT_CH], U8, align_bytes=64)
         nc.vector.memset(w_planes[:].bitcast(I32), 0)
@@ -49,18 +51,18 @@ def tile_fast2order_de_conv_kernel(tc, x, W_words, W_scales, out):
         def load_image(n):
             x_held.append(keep.tile([P, PIXELS], BF16, name="x_held%d" % n))
             x_window.append(keep.tile([P, GRID * SIDE], BF16, name="x_window%d" % n))
-            for jh in range(4):
-                rows = x_flat[n, :, SIDE * jh : SIDE * jh + GRID * SIDE]
-                nc.scalar.dma_start(
-                    out=x_window[n][jh:P:4, :],
-                    in_=rows.unsqueeze(1).to_broadcast([CHANNELS, 2, GRID * SIDE]),
-                )
             for iw0 in range(2):
                 for jh in range(4):
                     nc.sync.dma_start(
                         out=x_held[n][4 * iw0 + jh : P : 8, 0 : PIXELS - 1],
                         in_=x_flat[n, :, iw0 : iw0 + PIXELS - 1],
                     )
+            for jh in range(4):
+                rows = x_flat[n, :, SIDE * jh : SIDE * jh + GRID * SIDE]
+                nc.sync.dma_start(
+                    out=x_window[n][jh:P:4, :],
+                    in_=rows.unsqueeze(1).to_broadcast([CHANNELS, 2, GRID * SIDE]),
+                )
 
         load_image(0)
 
@@ -76,18 +78,23 @@ def tile_fast2order_de_conv_kernel(tc, x, W_words, W_scales, out):
         for a in range(PASSES):
             nc.sync.dma_start(out=w_words[:, a, :].bitcast(I32), in_=words_by_pass[a].bitcast(I32))
 
-        for n in range(1, IMAGES):
-            load_image(n)
-
         held = []
         windows = []
 
         def table_pieces(n):
             held.append(keep.tile([P, SHIFTS, SIDE * HELD_ROW], BF16, name="held%d" % n))
             windows.append(keep.tile([P, PHASES, GRID * GRID], BF16, name="windows%d" % n))
+            image_rows = x_held[n][:].rearrange("p (h w) -> p h w", w=SIDE)
             window_rows = x_window[n][:].rearrange("p (y w) -> p y w", w=SIDE)
-            held_rows = x_held[n][:].rearrange("p (h w) -> p h w", w=SIDE)
             pieces = []
+            for shift in range(SHIFTS):
+                every_fourth = image_rows[:, :, shift : shift + PACK * (QUADS - 1) + 1 : PACK]
+                pieces.append(
+                    (
+                        held[n][:, shift, :].rearrange("p (h q t) -> p h q t", q=QUADS, t=PACK),
+                        every_fourth.unsqueeze(3).to_broadcast([P, SIDE, QUADS, PACK]),
+                    )
+                )
             for phase in range(PHASES):
                 pieces.append(
                     (
@@ -95,32 +102,24 @@ def tile_fast2order_de_conv_kernel(tc, x, W_words, W_scales, out):
                         window_rows[:, :, phase : phase + GRID],
                     )
                 )
-            for shift in range(SHIFTS):
-                every_fourth = held_rows[:, :, shift : shift + PACK * (QUADS - 1) + 1 : PACK]
-                pieces.append(
-                    (
-                        held[n][:, shift, :].rearrange("p (h q t) -> p h q t", q=QUADS, t=PACK),
-                        every_fourth.unsqueeze(3).to_broadcast([P, SIDE, QUADS, PACK]),
-                    )
-                )
             return pieces
 
-        first_pieces = table_pieces(0)
-        for destination, source in first_pieces[: PHASES + PHASES]:
-            nc.vector.tensor_copy(out=destination, in_=source)
-        for destination, source in first_pieces[PHASES + PHASES :]:
-            nc.scalar.copy(out=destination, in_=source)
+        for piece, (destination, source) in enumerate(table_pieces(0)):
+            if PHASES <= piece < SHIFTS:
+                nc.scalar.copy(out=destination, in_=source)
+            else:
+                nc.vector.tensor_copy(out=destination, in_=source)
 
-        steps = [(n, half, a) for n in range(IMAGES) for half in range(TILES_PER_IMAGE) for a in range(PASSES)]
+        steps = [(n, a) for n in range(IMAGES) for a in range(PASSES)]
 
-        def multiply(n, half, a):
+        def multiply(n, a):
             ih, iwh = a // 2, a % 2
-            first_row = TILE_ROWS * half + ih
-            feat = feats.tile([P, PHASES, PACK * N_TILE // PHASES], BF16, name="feat", align_bytes=64)
+            feat = feats.tile([P, TILES_PER_IMAGE, PHASES, PACK * N_TILE // PHASES], BF16, name="feat", align_bytes=64)
+            held_part = held[n][:, 2 * iwh : 2 * iwh + PHASES, HELD_ROW * ih : HELD_ROW * (ih + GRID)]
             nc.vector.tensor_tensor(
                 out=feat[:],
-                in0=held[n][:, 2 * iwh : 2 * iwh + PHASES, HELD_ROW * first_row : HELD_ROW * (first_row + TILE_ROWS)],
-                in1=windows[n][:, :, GRID * TILE_ROWS * half : GRID * TILE_ROWS * (half + 1)],
+                in0=held_part.rearrange("p s (h e) -> p h s e", h=TILES_PER_IMAGE),
+                in1=windows[n][:].rearrange("p s (h e) -> p h s e", h=TILES_PER_IMAGE),
                 op=mybir.AluOpType.mult,
             )
             return feat
@@ -128,44 +127,47 @@ def tile_fast2order_de_conv_kernel(tc, x, W_words, W_scales, out):
         sums = []
         later_pieces = []
         feat_next = multiply(*steps[0])
-        for k, (n, half, a) in enumerate(steps):
+        for k, (n, a) in enumerate(steps):
+            if a == 0 and n + 1 < IMAGES:
+                load_image(n + 1)
+
             feat = feat_next
             if k + 1 < len(steps):
                 feat_next = multiply(*steps[k + 1])
-            codes = packed.tile([P, N_TILE], U32, name="codes", align_bytes=64)
-            scales = packed.tile([P, N_TILE], U8, name="scales", align_bytes=64)
+            codes = packed.tile([P, TILES_PER_IMAGE * N_TILE], U32, name="codes", align_bytes=64)
+            scales = packed.tile([P, TILES_PER_IMAGE * N_TILE], U8, name="scales", align_bytes=64)
             nc.vector.quantize_mx(
                 out=codes[:].bitcast(FP8X4),
                 scales=scales[:],
-                in_=feat[:].rearrange("p s e -> p (s e)"),
+                in_=feat[:].rearrange("p h s e -> p (h s e)"),
             )
 
+            banks = [(m, half) for m in range(M_TILES) for half in range(TILES_PER_IMAGE)]
             if a == 0:
-                sums = [psum.tile([P, N_TILE], F32, name="sums%d" % m) for m in range(M_TILES)]
-            for m in range(M_TILES):
+                sums = [psum.tile([P, N_TILE], F32, name="sums%d%d" % bank) for bank in banks]
+            for bank, (m, half) in enumerate(banks):
                 nc.tensor.matmul_mx(
-                    out=sums[m][:],
+                    out=sums[bank][:],
                     lhsT=w_words[:, a, 2 * P * m : 2 * P * (m + 1)].bitcast(FP4X4),
                     lhsT_scale=w_planes[:, a, P * m : P * (m + 1)],
-                    rhs=codes[:].bitcast(FP8X4),
-                    rhs_scale=scales[:],
+                    rhs=codes[:, N_TILE * half : N_TILE * (half + 1)].bitcast(FP8X4),
+                    rhs_scale=scales[:, N_TILE * half : N_TILE * (half + 1)],
                     start=(a == 0),
                     stop=(a == PASSES - 1),
                 )
 
-            if half == 0 and a == 0:
+            if a == 0:
                 later_pieces = table_pieces(n + 1) if n + 1 < IMAGES else []
-            step_in_image = PASSES * half + a
-            if step_in_image < len(later_pieces):
-                destination, source = later_pieces[step_in_image]
+            for destination, source in later_pieces[PIECES_PER_STEP * a : PIECES_PER_STEP * (a + 1)]:
                 nc.scalar.copy(out=destination, in_=source)
 
             if a == PASSES - 1:
-                for m in range(M_TILES):
+                emptiers = [nc.scalar.copy, nc.vector.tensor_copy] if k + 1 == len(steps) else [nc.scalar.copy]
+                for bank, (m, half) in enumerate(banks):
                     result = results.tile([P, TILE_ROWS, QUADS, PHASES], F32, name="result")
-                    nc.scalar.copy(
+                    emptiers[bank % len(emptiers)](
                         out=result[:],
-                        in_=sums[m][:].rearrange("o (s y q) -> o y q s", s=PHASES, y=TILE_ROWS),
+                        in_=sums[bank][:].rearrange("o (s y q) -> o y q s", s=PHASES, y=TILE_ROWS),
                     )
                     nc.sync.dma_start(
                         out=out[n, P * m : P * (m + 1), TILE_ROWS * half : TILE_ROWS * (half + 1), :].rearrange(

@@ -1,6 +1,7 @@
 from contextlib import ExitStack
 
 import concourse.mybir as mybir
+from concourse.masks import make_identity
 
 BF16 = mybir.dt.bfloat16
 F32 = mybir.dt.float32
@@ -27,6 +28,10 @@ TILES_PER_IMAGE = GRID // TILE_ROWS
 OUT_CH = 256
 M_TILES = OUT_CH // P
 HELD_ROW = QUADS * PACK
+VECTOR_ROWS = 13
+VECTOR_PART = VECTOR_ROWS * GRID
+GPSIMD_PART = (TILE_ROWS - VECTOR_ROWS) * GRID
+PHASES_PER_BANK = 2
 PIECES_PER_STEP = 2
 FLOPS = 2 * IMAGES * GRID * GRID * CHANNELS * 256 * OUT_CH
 
@@ -39,7 +44,10 @@ def tile_fast2order_de_conv_kernel(tc, x, W_words, W_scales, out):
         feats = ctx.enter_context(tc.tile_pool(name="feats", bufs=3))
         packed = ctx.enter_context(tc.tile_pool(name="packed", bufs=4))
         results = ctx.enter_context(tc.tile_pool(name="results", bufs=4))
-        psum = ctx.enter_context(tc.psum_pool(name="psum", bufs=2))
+        psum = ctx.enter_context(tc.psum_pool(name="psum", bufs=1))
+
+        identity = keep.tile([P, P], BF16)
+        make_identity(nc, identity[:])
 
         w_planes = keep.tile([P, PASSES, OUT_CH], U8, align_bytes=64)
         nc.vector.memset(w_planes[:].bitcast(I32), 0)
@@ -79,13 +87,31 @@ def tile_fast2order_de_conv_kernel(tc, x, W_words, W_scales, out):
             nc.sync.dma_start(out=w_words[:, a, :].bitcast(I32), in_=words_by_pass[a].bitcast(I32))
 
         held = []
-        windows = []
+        window_tails = []
+
+        def fill_window_banks(n):
+            window_rows = x_window[n][:].rearrange("p (y w) -> p y w", w=SIDE)
+            banks = []
+            for half in range(TILES_PER_IMAGE):
+                for pair in range(PHASES // PHASES_PER_BANK):
+                    bank = psum.tile([P, PHASES_PER_BANK, N_TILE], BF16, name="window_bank%d%d" % (half, pair))
+                    for s in range(PHASES_PER_BANK):
+                        phase = PHASES_PER_BANK * pair + s
+                        nc.tensor.matmul(
+                            out=bank[:, s, :].rearrange("p (y u) -> p y u", u=GRID),
+                            lhsT=identity[:],
+                            rhs=window_rows[:, TILE_ROWS * half : TILE_ROWS * (half + 1), phase : phase + GRID],
+                            start=True,
+                            stop=True,
+                        )
+                    banks.append(bank)
+            return banks
 
         def table_pieces(n):
             held.append(keep.tile([P, SHIFTS, SIDE * HELD_ROW], BF16, name="held%d" % n))
-            windows.append(keep.tile([P, PHASES, GRID * GRID], BF16, name="windows%d" % n))
+            window_tails.append(keep.tile([P, TILES_PER_IMAGE, PHASES, GPSIMD_PART], BF16, name="window_tails%d" % n))
             image_rows = x_held[n][:].rearrange("p (h w) -> p h w", w=SIDE)
-            window_rows = x_window[n][:].rearrange("p (y w) -> p y w", w=SIDE)
+            tile_rows = x_window[n][:].rearrange("p (h y w) -> p h y w", h=TILES_PER_IMAGE, w=SIDE)
             pieces = []
             for shift in range(SHIFTS):
                 every_fourth = image_rows[:, :, shift : shift + PACK * (QUADS - 1) + 1 : PACK]
@@ -98,28 +124,40 @@ def tile_fast2order_de_conv_kernel(tc, x, W_words, W_scales, out):
             for phase in range(PHASES):
                 pieces.append(
                     (
-                        windows[n][:, phase, :].rearrange("p (y u) -> p y u", u=GRID),
-                        window_rows[:, :, phase : phase + GRID],
+                        window_tails[n][:, :, phase, :].rearrange("p h (y u) -> p h y u", u=GRID),
+                        tile_rows[:, :, VECTOR_ROWS:TILE_ROWS, phase : phase + GRID],
                     )
                 )
             return pieces
 
+        window_banks = fill_window_banks(0)
         for piece, (destination, source) in enumerate(table_pieces(0)):
-            if PHASES <= piece < SHIFTS:
-                nc.scalar.copy(out=destination, in_=source)
-            else:
+            if piece < PHASES:
                 nc.vector.tensor_copy(out=destination, in_=source)
+            else:
+                nc.scalar.copy(out=destination, in_=source)
 
         steps = [(n, a) for n in range(IMAGES) for a in range(PASSES)]
 
         def multiply(n, a):
             ih, iwh = a // 2, a % 2
             feat = feats.tile([P, TILES_PER_IMAGE, PHASES, PACK * N_TILE // PHASES], BF16, name="feat", align_bytes=64)
-            held_part = held[n][:, 2 * iwh : 2 * iwh + PHASES, HELD_ROW * ih : HELD_ROW * (ih + GRID)]
-            nc.vector.tensor_tensor(
-                out=feat[:],
-                in0=held_part.rearrange("p s (h e) -> p h s e", h=TILES_PER_IMAGE),
-                in1=windows[n][:].rearrange("p s (h e) -> p h s e", h=TILES_PER_IMAGE),
+            held_part = held[n][:, 2 * iwh : 2 * iwh + PHASES, HELD_ROW * ih : HELD_ROW * (ih + GRID)].rearrange(
+                "p s (h e) -> p h s e", h=TILES_PER_IMAGE
+            )
+            for half in range(TILES_PER_IMAGE):
+                for pair in range(PHASES // PHASES_PER_BANK):
+                    phases = slice(PHASES_PER_BANK * pair, PHASES_PER_BANK * (pair + 1))
+                    nc.vector.tensor_tensor(
+                        out=feat[:, half, phases, 0:VECTOR_PART],
+                        in0=held_part[:, half, phases, 0:VECTOR_PART],
+                        in1=window_banks[(PHASES // PHASES_PER_BANK) * half + pair][:, :, 0:VECTOR_PART],
+                        op=mybir.AluOpType.mult,
+                    )
+            nc.gpsimd.tensor_tensor(
+                out=feat[:, :, :, VECTOR_PART:],
+                in0=held_part[:, :, :, VECTOR_PART:],
+                in1=window_tails[n][:],
                 op=mybir.AluOpType.mult,
             )
             return feat
@@ -134,6 +172,8 @@ def tile_fast2order_de_conv_kernel(tc, x, W_words, W_scales, out):
             feat = feat_next
             if k + 1 < len(steps):
                 feat_next = multiply(*steps[k + 1])
+            if a == PASSES - 2 and n + 1 < IMAGES:
+                window_banks = fill_window_banks(n + 1)
             codes = packed.tile([P, TILES_PER_IMAGE * N_TILE], U32, name="codes", align_bytes=64)
             scales = packed.tile([P, TILES_PER_IMAGE * N_TILE], U8, name="scales", align_bytes=64)
             nc.vector.quantize_mx(

@@ -32,6 +32,7 @@ VECTOR_ROWS = 13
 VECTOR_PART = VECTOR_ROWS * GRID
 GPSIMD_PART = (TILE_ROWS - VECTOR_ROWS) * GRID
 PHASES_PER_BANK = 2
+FEAT_BUFS = 5
 PIECES_PER_STEP = 2
 FLOPS = 2 * IMAGES * GRID * GRID * CHANNELS * 256 * OUT_CH
 
@@ -41,7 +42,7 @@ def tile_fast2order_de_conv_kernel(tc, x, W_words, W_scales, out):
     with ExitStack() as ctx:
         ctx.enter_context(tc.manual_schedule())
         keep = ctx.enter_context(tc.tile_pool(name="keep", bufs=1))
-        feats = ctx.enter_context(tc.tile_pool(name="feats", bufs=3))
+        feats = ctx.enter_context(tc.tile_pool(name="feats", bufs=FEAT_BUFS))
         packed = ctx.enter_context(tc.tile_pool(name="packed", bufs=4))
         results = ctx.enter_context(tc.tile_pool(name="results", bufs=4))
         psum = ctx.enter_context(tc.psum_pool(name="psum", bufs=1))

@@ -1,7 +1,6 @@
 from contextlib import ExitStack
 
 import concourse.mybir as mybir
-from concourse.masks import make_identity
 
 BF16 = mybir.dt.bfloat16
 F32 = mybir.dt.float32
@@ -27,13 +26,12 @@ N_TILE = TILE_ROWS * GRID
 TILES_PER_IMAGE = GRID // TILE_ROWS
 OUT_CH = 256
 M_TILES = OUT_CH // P
-HELD_ROW = QUADS * PACK
-VECTOR_ROWS = 13
-VECTOR_PART = VECTOR_ROWS * GRID
-GPSIMD_PART = (TILE_ROWS - VECTOR_ROWS) * GRID
-PHASES_PER_BANK = 2
-FEAT_BUFS = 5
-PIECES_PER_STEP = 2
+ROW = GRID * PACK
+IMAGE_COLS = GRID * ROW
+A_ROWS = GRID + 2
+B_ROWS = GRID
+OWN_ROWS = 2
+WIN_ROWS = A_ROWS
 FLOPS = 2 * IMAGES * GRID * GRID * CHANNELS * 256 * OUT_CH
 
 
@@ -42,35 +40,34 @@ def tile_fast2order_de_conv_kernel(tc, x, W_words, W_scales, out):
     with ExitStack() as ctx:
         ctx.enter_context(tc.manual_schedule())
         keep = ctx.enter_context(tc.tile_pool(name="keep", bufs=1))
-        feats = ctx.enter_context(tc.tile_pool(name="feats", bufs=FEAT_BUFS))
+        tables = ctx.enter_context(tc.tile_pool(name="tables", bufs=2))
+        prods = ctx.enter_context(tc.tile_pool(name="prods", bufs=3))
+        moved = ctx.enter_context(tc.tile_pool(name="moved", bufs=3))
         packed = ctx.enter_context(tc.tile_pool(name="packed", bufs=4))
         results = ctx.enter_context(tc.tile_pool(name="results", bufs=4))
-        psum = ctx.enter_context(tc.psum_pool(name="psum", bufs=1))
+        psum = ctx.enter_context(tc.psum_pool(name="psum", bufs=2))
 
-        identity = keep.tile([P, P], BF16)
-        make_identity(nc, identity[:])
-
+        x_flat = x.rearrange("n c h w -> n c (h w)")
+        x_held = [keep.tile([P, PIXELS], BF16, name="x_held%d" % b) for b in range(2)]
+        x_rows = [keep.tile([P, WIN_ROWS * SIDE], BF16, name="x_rows%d" % b) for b in range(2)]
+        nc.vector.memset(x_rows[0][:], 0.0)
+        nc.gpsimd.memset(x_rows[1][:], 0.0)
         w_planes = keep.tile([P, PASSES, OUT_CH], U8, align_bytes=64)
         nc.vector.memset(w_planes[:].bitcast(I32), 0)
 
-        x_flat = x.rearrange("n c h w -> n c (h w)")
-        x_held = []
-        x_window = []
-
         def load_image(n):
-            x_held.append(keep.tile([P, PIXELS], BF16, name="x_held%d" % n))
-            x_window.append(keep.tile([P, GRID * SIDE], BF16, name="x_window%d" % n))
             for iw0 in range(2):
                 for jh in range(4):
                     nc.sync.dma_start(
-                        out=x_held[n][4 * iw0 + jh : P : 8, 0 : PIXELS - 1],
+                        out=x_held[n % 2][4 * iw0 + jh : P : 8, 0 : PIXELS - 1],
                         in_=x_flat[n, :, iw0 : iw0 + PIXELS - 1],
                     )
             for jh in range(4):
-                rows = x_flat[n, :, SIDE * jh : SIDE * jh + GRID * SIDE]
+                count = min(WIN_ROWS, SIDE - jh)
+                rows = x_flat[n, :, SIDE * jh : SIDE * (jh + count)]
                 nc.sync.dma_start(
-                    out=x_window[n][jh:P:4, :],
-                    in_=rows.unsqueeze(1).to_broadcast([CHANNELS, 2, GRID * SIDE]),
+                    out=x_rows[n % 2][jh:P:4, 0 : SIDE * count],
+                    in_=rows.unsqueeze(1).to_broadcast([CHANNELS, 2, SIDE * count]),
                 )
 
         load_image(0)
@@ -81,138 +78,139 @@ def tile_fast2order_de_conv_kernel(tc, x, W_words, W_scales, out):
                 out=w_planes[32 * quadrant : 32 * quadrant + 4].rearrange("p a o -> p (a o)").bitcast(I32),
                 in_=scale_rows[4 * quadrant : 4 * quadrant + 4, :].bitcast(I32),
             )
-
         w_words = keep.tile([P, PASSES, 2 * OUT_CH], U8, align_bytes=64)
         words_by_pass = W_words.rearrange("g (c2 a r) b -> a (g c2) r b", c2=2, a=PASSES)
         for a in range(PASSES):
             nc.sync.dma_start(out=w_words[:, a, :].bitcast(I32), in_=words_by_pass[a].bitcast(I32))
 
-        held = []
-        window_tails = []
+        load_image(1)
 
-        def fill_window_banks(n):
-            window_rows = x_window[n][:].rearrange("p (y w) -> p y w", w=SIDE)
-            banks = []
-            for half in range(TILES_PER_IMAGE):
-                for pair in range(PHASES // PHASES_PER_BANK):
-                    bank = psum.tile([P, PHASES_PER_BANK, N_TILE], BF16, name="window_bank%d%d" % (half, pair))
-                    for s in range(PHASES_PER_BANK):
-                        phase = PHASES_PER_BANK * pair + s
-                        nc.tensor.matmul(
-                            out=bank[:, s, :].rearrange("p (y u) -> p y u", u=GRID),
-                            lhsT=identity[:],
-                            rhs=window_rows[:, TILE_ROWS * half : TILE_ROWS * (half + 1), phase : phase + GRID],
-                            start=True,
-                            stop=True,
-                        )
-                    banks.append(bank)
-            return banks
+        held = {}
+        wins = {}
 
         def table_pieces(n):
-            held.append(keep.tile([P, SHIFTS, SIDE * HELD_ROW], BF16, name="held%d" % n))
-            window_tails.append(keep.tile([P, TILES_PER_IMAGE, PHASES, GPSIMD_PART], BF16, name="window_tails%d" % n))
-            image_rows = x_held[n][:].rearrange("p (h w) -> p h w", w=SIDE)
-            tile_rows = x_window[n][:].rearrange("p (h y w) -> p h y w", h=TILES_PER_IMAGE, w=SIDE)
+            held[n] = tables.tile([P, SIDE, SHIFTS * GRID], BF16, name="held")
+            wins[n] = tables.tile([P, WIN_ROWS, ROW], BF16, name="wins")
+            image_rows = x_held[n % 2][:].rearrange("p (h w) -> p h w", w=SIDE)
+            window_rows = x_rows[n % 2][:].rearrange("p (r w) -> p r w", w=SIDE)
             pieces = []
             for shift in range(SHIFTS):
                 every_fourth = image_rows[:, :, shift : shift + PACK * (QUADS - 1) + 1 : PACK]
                 pieces.append(
                     (
-                        held[n][:, shift, :].rearrange("p (h q t) -> p h q t", q=QUADS, t=PACK),
+                        held[n][:, :, GRID * shift : GRID * (shift + 1)].rearrange("p h (q t) -> p h q t", t=PACK),
                         every_fourth.unsqueeze(3).to_broadcast([P, SIDE, QUADS, PACK]),
                     )
                 )
             for phase in range(PHASES):
                 pieces.append(
-                    (
-                        window_tails[n][:, :, phase, :].rearrange("p h (y u) -> p h y u", u=GRID),
-                        tile_rows[:, :, VECTOR_ROWS:TILE_ROWS, phase : phase + GRID],
-                    )
+                    (wins[n][:, :, GRID * phase : GRID * (phase + 1)], window_rows[:, :, phase : phase + GRID])
                 )
             return pieces
 
-        window_banks = fill_window_banks(0)
-        for piece, (destination, source) in enumerate(table_pieces(0)):
-            if piece < PHASES:
-                nc.vector.tensor_copy(out=destination, in_=source)
-            else:
-                nc.scalar.copy(out=destination, in_=source)
+        products = {}
 
-        steps = [(n, a) for n in range(IMAGES) for a in range(PASSES)]
-
-        def multiply(n, a):
-            ih, iwh = a // 2, a % 2
-            feat = feats.tile([P, TILES_PER_IMAGE, PHASES, PACK * N_TILE // PHASES], BF16, name="feat", align_bytes=64)
-            held_part = held[n][:, 2 * iwh : 2 * iwh + PHASES, HELD_ROW * ih : HELD_ROW * (ih + GRID)].rearrange(
-                "p s (h e) -> p h s e", h=TILES_PER_IMAGE
-            )
-            for half in range(TILES_PER_IMAGE):
-                for pair in range(PHASES // PHASES_PER_BANK):
-                    phases = slice(PHASES_PER_BANK * pair, PHASES_PER_BANK * (pair + 1))
-                    nc.vector.tensor_tensor(
-                        out=feat[:, half, phases, 0:VECTOR_PART],
-                        in0=held_part[:, half, phases, 0:VECTOR_PART],
-                        in1=window_banks[(PHASES // PHASES_PER_BANK) * half + pair][:, :, 0:VECTOR_PART],
-                        op=mybir.AluOpType.mult,
-                    )
-            nc.gpsimd.tensor_tensor(
-                out=feat[:, :, :, VECTOR_PART:],
-                in0=held_part[:, :, :, VECTOR_PART:],
-                in1=window_tails[n][:],
+        def multiply(n, iwh):
+            ta = prods.tile([P, A_ROWS * ROW], BF16, name="ta", align_bytes=64)
+            tb = prods.tile([P, B_ROWS * ROW], BF16, name="tb", align_bytes=64)
+            f = moved.tile([P, 2, IMAGE_COLS], BF16, name="f", align_bytes=64)
+            shifts = slice(2 * GRID * iwh, 2 * GRID * iwh + ROW)
+            nc.vector.tensor_tensor(
+                out=ta[:].rearrange("p (u e) -> p u e", e=ROW),
+                in0=held[n][:, 0:A_ROWS, shifts],
+                in1=wins[n][:, 0:A_ROWS, :],
                 op=mybir.AluOpType.mult,
             )
-            return feat
-
-        sums = []
-        later_pieces = []
-        feat_next = multiply(*steps[0])
-        for k, (n, a) in enumerate(steps):
-            if a == 0 and n + 1 < IMAGES:
-                load_image(n + 1)
-
-            feat = feat_next
-            if k + 1 < len(steps):
-                feat_next = multiply(*steps[k + 1])
-            if a == PASSES - 2 and n + 1 < IMAGES:
-                window_banks = fill_window_banks(n + 1)
-            codes = packed.tile([P, TILES_PER_IMAGE * N_TILE], U32, name="codes", align_bytes=64)
-            scales = packed.tile([P, TILES_PER_IMAGE * N_TILE], U8, name="scales", align_bytes=64)
-            nc.vector.quantize_mx(
-                out=codes[:].bitcast(FP8X4),
-                scales=scales[:],
-                in_=feat[:].rearrange("p h s e -> p (h s e)"),
+            nc.vector.tensor_tensor(
+                out=tb[:].rearrange("p (u e) -> p u e", e=ROW),
+                in0=held[n][:, 3 : 3 + B_ROWS, shifts],
+                in1=wins[n][:, 0:B_ROWS, :],
+                op=mybir.AluOpType.mult,
             )
+            for ih in (1, 2):
+                nc.vector.tensor_tensor(
+                    out=f[:, ih - 1, 0 : OWN_ROWS * ROW].rearrange("p (u e) -> p u e", e=ROW),
+                    in0=held[n][:, ih : ih + OWN_ROWS, shifts],
+                    in1=wins[n][:, 0:OWN_ROWS, :],
+                    op=mybir.AluOpType.mult,
+                )
+            rows = GRID - OWN_ROWS
+            rest = slice(OWN_ROWS * ROW, IMAGE_COLS)
+            for jh in range(1, 4):
+                nc.sync.dma_start(out=f[jh:P:4, 0, rest], in_=ta[jh - 1 : P : 4, 3 * ROW : (3 + rows) * ROW])
+            nc.sync.dma_start(out=f[0:P:4, 0, rest], in_=tb[2:P:4, 0 : rows * ROW])
+            for jh in range(3):
+                nc.sync.dma_start(out=f[jh:P:4, 1, rest], in_=tb[jh + 1 : P : 4, ROW : (1 + rows) * ROW])
+            nc.sync.dma_start(out=f[3:P:4, 1, rest], in_=ta[1:P:4, 4 * ROW : (4 + rows) * ROW])
+            products[(n, iwh)] = {0: ta[:, 0:IMAGE_COLS], 1: f[:, 0, :], 2: f[:, 1, :], 3: tb[:]}
 
-            banks = [(m, half) for m in range(M_TILES) for half in range(TILES_PER_IMAGE)]
-            if a == 0:
-                sums = [psum.tile([P, N_TILE], F32, name="sums%d%d" % bank) for bank in banks]
+        banks = [(m, half) for m in range(M_TILES) for half in range(TILES_PER_IMAGE)]
+        sums = {}
+        done = {}
+
+        def contract(n, ih, iwh):
+            a = 2 * ih + iwh
+            codes = packed.tile([P, IMAGE_COLS // PACK], U32, name="codes", align_bytes=64)
+            scales = packed.tile([P, IMAGE_COLS // PACK], U8, name="scales", align_bytes=64)
+            nc.vector.quantize_mx(out=codes[:].bitcast(FP8X4), scales=scales[:], in_=products[(n, iwh)][ih])
+            if n not in sums:
+                sums[n] = [psum.tile([P, N_TILE], F32, name="sums%d%d" % bank) for bank in banks]
+                done[n] = 0
             for bank, (m, half) in enumerate(banks):
                 nc.tensor.matmul_mx(
-                    out=sums[bank][:],
+                    out=sums[n][bank][:],
                     lhsT=w_words[:, a, 2 * P * m : 2 * P * (m + 1)].bitcast(FP4X4),
                     lhsT_scale=w_planes[:, a, P * m : P * (m + 1)],
                     rhs=codes[:, N_TILE * half : N_TILE * (half + 1)].bitcast(FP8X4),
                     rhs_scale=scales[:, N_TILE * half : N_TILE * (half + 1)],
-                    start=(a == 0),
-                    stop=(a == PASSES - 1),
+                    start=(done[n] == 0),
+                    stop=(done[n] == PASSES - 1),
+                )
+            done[n] += 1
+
+        def empty(n):
+            emptiers = [nc.scalar.copy, nc.vector.tensor_copy] if n + 1 == IMAGES else [nc.scalar.copy]
+            for bank, (m, half) in enumerate(banks):
+                result = results.tile([P, TILE_ROWS, QUADS, PHASES], F32, name="result")
+                emptiers[bank % len(emptiers)](
+                    out=result[:],
+                    in_=sums[n][bank][:].rearrange("o (y s q) -> o y q s", s=PHASES, y=TILE_ROWS),
+                )
+                nc.sync.dma_start(
+                    out=out[n, P * m : P * (m + 1), TILE_ROWS * half : TILE_ROWS * (half + 1), :].rearrange(
+                        "o y z -> o (y z)"
+                    ),
+                    in_=result[:].rearrange("o y q s -> o (y q s)"),
                 )
 
-            if a == 0:
-                later_pieces = table_pieces(n + 1) if n + 1 < IMAGES else []
-            for destination, source in later_pieces[PIECES_PER_STEP * a : PIECES_PER_STEP * (a + 1)]:
-                nc.scalar.copy(out=destination, in_=source)
+        first_pieces = table_pieces(0)
+        for destination, source in first_pieces[0:PHASES] + first_pieces[SHIFTS : SHIFTS + 1]:
+            nc.vector.tensor_copy(out=destination, in_=source)
+        for destination, source in first_pieces[SHIFTS + 1 :] + first_pieces[PHASES:SHIFTS]:
+            nc.scalar.copy(out=destination, in_=source)
 
-            if a == PASSES - 1:
-                emptiers = [nc.scalar.copy, nc.vector.tensor_copy] if k + 1 == len(steps) else [nc.scalar.copy]
-                for bank, (m, half) in enumerate(banks):
-                    result = results.tile([P, TILE_ROWS, QUADS, PHASES], F32, name="result")
-                    emptiers[bank % len(emptiers)](
-                        out=result[:],
-                        in_=sums[bank][:].rearrange("o (s y q) -> o y q s", s=PHASES, y=TILE_ROWS),
-                    )
-                    nc.sync.dma_start(
-                        out=out[n, P * m : P * (m + 1), TILE_ROWS * half : TILE_ROWS * (half + 1), :].rearrange(
-                            "o y z -> o (y z)"
-                        ),
-                        in_=result[:].rearrange("o y q s -> o (y q s)"),
-                    )
+        for destination, source in table_pieces(1):
+            nc.scalar.copy(out=destination, in_=source)
+        load_image(2)
+        multiply(0, 0)
+        multiply(0, 1)
+        for iwh in range(2):
+            contract(0, 0, iwh)
+            contract(0, 3, iwh)
+
+        for n in range(IMAGES):
+            if n + 2 < IMAGES:
+                for destination, source in table_pieces(n + 2):
+                    nc.scalar.copy(out=destination, in_=source)
+            if n + 3 < IMAGES:
+                load_image(n + 3)
+            for iwh in range(2):
+                if n + 1 < IMAGES:
+                    multiply(n + 1, iwh)
+                contract(n, 1, iwh)
+                contract(n, 2, iwh)
+            empty(n)
+            if n + 1 < IMAGES:
+                for iwh in range(2):
+                    contract(n + 1, 0, iwh)
+                    contract(n + 1, 3, iwh)

@@ -23,14 +23,14 @@ PASSES = 8
 SHIFTS = PHASES + 2
 TILE_ROWS = 16
 N_TILE = TILE_ROWS * GRID
-TILES_PER_IMAGE = GRID // TILE_ROWS
+HALVES = GRID // TILE_ROWS
 OUT_CH = 256
 M_TILES = OUT_CH // P
 ROW = GRID * PACK
 IMAGE_COLS = GRID * ROW
 A_ROWS = GRID + 2
 B_ROWS = GRID
-OWN_ROWS = 2
+OWN_ROWS = {1: 2, 2: 1}
 WIN_ROWS = A_ROWS
 FLOPS = 2 * IMAGES * GRID * GRID * CHANNELS * 256 * OUT_CH
 
@@ -51,6 +51,9 @@ def tile_fast2order_de_conv_kernel(tc, x, W_words, W_scales, out):
         x_held = [keep.tile([P, PIXELS], BF16, name="x_held%d" % b) for b in range(2)]
         x_rows = [keep.tile([P, WIN_ROWS * SIDE], BF16, name="x_rows%d" % b) for b in range(2)]
         nc.vector.memset(x_rows[0][:], 0.0)
+        warm = keep.tile([P, 2, 8], BF16)
+        nc.gpsimd.memset(warm[:, 0, :], 0.0)
+        nc.scalar.copy(out=warm[:, 1, :], in_=warm[:, 0, :])
         nc.gpsimd.memset(x_rows[1][:], 0.0)
         w_planes = keep.tile([P, PASSES, OUT_CH], U8, align_bytes=64)
         nc.vector.memset(w_planes[:].bitcast(I32), 0)
@@ -129,52 +132,54 @@ def tile_fast2order_de_conv_kernel(tc, x, W_words, W_scales, out):
             )
             for ih in (1, 2):
                 nc.vector.tensor_tensor(
-                    out=f[:, ih - 1, 0 : OWN_ROWS * ROW].rearrange("p (u e) -> p u e", e=ROW),
-                    in0=held[n][:, ih : ih + OWN_ROWS, shifts],
-                    in1=wins[n][:, 0:OWN_ROWS, :],
+                    out=f[:, ih - 1, 0 : OWN_ROWS[ih] * ROW].rearrange("p (u e) -> p u e", e=ROW),
+                    in0=held[n][:, ih : ih + OWN_ROWS[ih], shifts],
+                    in1=wins[n][:, 0 : OWN_ROWS[ih], :],
                     op=mybir.AluOpType.mult,
                 )
-            rows = GRID - OWN_ROWS
-            rest = slice(OWN_ROWS * ROW, IMAGE_COLS)
             for jh in range(1, 4):
-                nc.sync.dma_start(out=f[jh:P:4, 0, rest], in_=ta[jh - 1 : P : 4, 3 * ROW : (3 + rows) * ROW])
-            nc.sync.dma_start(out=f[0:P:4, 0, rest], in_=tb[2:P:4, 0 : rows * ROW])
+                nc.sync.dma_start(out=f[jh:P:4, 0, 2 * ROW :], in_=ta[jh - 1 : P : 4, 3 * ROW : (GRID + 1) * ROW])
+            nc.sync.dma_start(out=f[0:P:4, 0, 2 * ROW :], in_=tb[2:P:4, 0 : (GRID - 2) * ROW])
             for jh in range(3):
-                nc.sync.dma_start(out=f[jh:P:4, 1, rest], in_=tb[jh + 1 : P : 4, ROW : (1 + rows) * ROW])
-            nc.sync.dma_start(out=f[3:P:4, 1, rest], in_=ta[1:P:4, 4 * ROW : (4 + rows) * ROW])
+                nc.sync.dma_start(out=f[jh:P:4, 1, ROW:], in_=tb[jh + 1 : P : 4, 0 : (GRID - 1) * ROW])
+            nc.sync.dma_start(out=f[3:P:4, 1, ROW:], in_=ta[1:P:4, 3 * ROW : (GRID + 2) * ROW])
             products[(n, iwh)] = {0: ta[:, 0:IMAGE_COLS], 1: f[:, 0, :], 2: f[:, 1, :], 3: tb[:]}
 
-        banks = [(m, half) for m in range(M_TILES) for half in range(TILES_PER_IMAGE)]
         sums = {}
         done = {}
 
-        def contract(n, ih, iwh):
+        def contract(n, ih, iwh, halves):
             a = 2 * ih + iwh
-            codes = packed.tile([P, IMAGE_COLS // PACK], U32, name="codes", align_bytes=64)
-            scales = packed.tile([P, IMAGE_COLS // PACK], U8, name="scales", align_bytes=64)
-            nc.vector.quantize_mx(out=codes[:].bitcast(FP8X4), scales=scales[:], in_=products[(n, iwh)][ih])
-            if n not in sums:
-                sums[n] = [psum.tile([P, N_TILE], F32, name="sums%d%d" % bank) for bank in banks]
-                done[n] = 0
-            for bank, (m, half) in enumerate(banks):
-                nc.tensor.matmul_mx(
-                    out=sums[n][bank][:],
-                    lhsT=w_words[:, a, 2 * P * m : 2 * P * (m + 1)].bitcast(FP4X4),
-                    lhsT_scale=w_planes[:, a, P * m : P * (m + 1)],
-                    rhs=codes[:, N_TILE * half : N_TILE * (half + 1)].bitcast(FP8X4),
-                    rhs_scale=scales[:, N_TILE * half : N_TILE * (half + 1)],
-                    start=(done[n] == 0),
-                    stop=(done[n] == PASSES - 1),
-                )
-            done[n] += 1
+            width = len(halves) * N_TILE
+            codes = packed.tile([P, HALVES * N_TILE], U32, name="codes", align_bytes=64)
+            scales = packed.tile([P, HALVES * N_TILE], U8, name="scales", align_bytes=64)
+            nc.vector.quantize_mx(
+                out=codes[:, 0:width].bitcast(FP8X4),
+                scales=scales[:, 0:width],
+                in_=products[(n, iwh)][ih][:, PACK * N_TILE * halves[0] : PACK * N_TILE * (halves[-1] + 1)],
+            )
+            for place, half in enumerate(halves):
+                for m in range(M_TILES):
+                    if (n, half, m) not in sums:
+                        sums[(n, half, m)] = psum.tile([P, N_TILE], F32, name="sums%d%d" % (half, m))
+                        done[(n, half, m)] = 0
+                    nc.tensor.matmul_mx(
+                        out=sums[(n, half, m)][:],
+                        lhsT=w_words[:, a, 2 * P * m : 2 * P * (m + 1)].bitcast(FP4X4),
+                        lhsT_scale=w_planes[:, a, P * m : P * (m + 1)],
+                        rhs=codes[:, N_TILE * place : N_TILE * (place + 1)].bitcast(FP8X4),
+                        rhs_scale=scales[:, N_TILE * place : N_TILE * (place + 1)],
+                        start=(done[(n, half, m)] == 0),
+                        stop=(done[(n, half, m)] == PASSES - 1),
+                    )
+                    done[(n, half, m)] += 1
 
-        def empty(n):
-            emptiers = [nc.scalar.copy, nc.vector.tensor_copy] if n + 1 == IMAGES else [nc.scalar.copy]
-            for bank, (m, half) in enumerate(banks):
+        def empty(n, half, emptiers):
+            for m in range(M_TILES):
                 result = results.tile([P, TILE_ROWS, QUADS, PHASES], F32, name="result")
-                emptiers[bank % len(emptiers)](
+                emptiers[m % len(emptiers)](
                     out=result[:],
-                    in_=sums[n][bank][:].rearrange("o (y s q) -> o y q s", s=PHASES, y=TILE_ROWS),
+                    in_=sums[(n, half, m)][:].rearrange("o (y s q) -> o y q s", s=PHASES, y=TILE_ROWS),
                 )
                 nc.sync.dma_start(
                     out=out[n, P * m : P * (m + 1), TILE_ROWS * half : TILE_ROWS * (half + 1), :].rearrange(
@@ -183,34 +188,47 @@ def tile_fast2order_de_conv_kernel(tc, x, W_words, W_scales, out):
                     in_=result[:].rearrange("o y q s -> o (y q s)"),
                 )
 
-        first_pieces = table_pieces(0)
-        for destination, source in first_pieces[0:PHASES] + first_pieces[SHIFTS : SHIFTS + 1]:
-            nc.vector.tensor_copy(out=destination, in_=source)
-        for destination, source in first_pieces[SHIFTS + 1 :] + first_pieces[PHASES:SHIFTS]:
-            nc.scalar.copy(out=destination, in_=source)
+        both = list(range(HALVES))
 
+        first_pieces = table_pieces(0)
+        for destination, source in first_pieces[3:PHASES] + first_pieces[SHIFTS:]:
+            nc.vector.tensor_copy(out=destination, in_=source)
+        for destination, source in first_pieces[0:3] + first_pieces[PHASES:SHIFTS]:
+            nc.scalar.copy(out=destination, in_=source)
         for destination, source in table_pieces(1):
             nc.scalar.copy(out=destination, in_=source)
-        load_image(2)
+
         multiply(0, 0)
         multiply(0, 1)
+        load_image(2)
         for iwh in range(2):
-            contract(0, 0, iwh)
-            contract(0, 3, iwh)
+            contract(0, 0, iwh, both)
+            contract(0, 3, iwh, both)
 
         for n in range(IMAGES):
+            last = n + 1 == IMAGES
             if n + 2 < IMAGES:
                 for destination, source in table_pieces(n + 2):
                     nc.scalar.copy(out=destination, in_=source)
             if n + 3 < IMAGES:
                 load_image(n + 3)
-            for iwh in range(2):
-                if n + 1 < IMAGES:
-                    multiply(n + 1, iwh)
-                contract(n, 1, iwh)
-                contract(n, 2, iwh)
-            empty(n)
-            if n + 1 < IMAGES:
+            if not last:
+                multiply(n + 1, 0)
+            contract(n, 1, 0, both)
+            contract(n, 2, 0, both)
+            if not last:
+                multiply(n + 1, 1)
+                contract(n, 1, 1, both)
+                contract(n, 2, 1, both)
+                for half in both:
+                    empty(n, half, [nc.scalar.copy])
                 for iwh in range(2):
-                    contract(n + 1, 0, iwh)
-                    contract(n + 1, 3, iwh)
+                    contract(n + 1, 0, iwh, both)
+                    contract(n + 1, 3, iwh, both)
+            else:
+                contract(n, 1, 1, [0])
+                contract(n, 2, 1, [0])
+                empty(n, 0, [nc.scalar.copy])
+                contract(n, 1, 1, [1])
+                contract(n, 2, 1, [1])
+                empty(n, 1, [nc.scalar.copy, nc.vector.tensor_copy])

@@ -28,10 +28,11 @@ OUT_CH = 256
 M_TILES = OUT_CH // P
 ROW = GRID * PACK
 IMAGE_COLS = GRID * ROW
-A_ROWS = GRID + 2
-B_ROWS = GRID
-OWN_ROWS = {1: 2, 2: 1}
-WIN_ROWS = A_ROWS
+T_ROWS = GRID + 2
+TOP_ROWS = 2
+TOP_PITCH = 48
+LOW_ROWS = T_ROWS
+WIN_ROWS = TOP_ROWS + LOW_ROWS
 FLOPS = 2 * IMAGES * GRID * GRID * CHANNELS * 256 * OUT_CH
 
 
@@ -49,12 +50,15 @@ def tile_fast2order_de_conv_kernel(tc, x, W_words, W_scales, out):
 
         x_flat = x.rearrange("n c h w -> n c (h w)")
         x_held = [keep.tile([P, PIXELS], BF16, name="x_held%d" % b) for b in range(2)]
-        x_rows = [keep.tile([P, WIN_ROWS * SIDE], BF16, name="x_rows%d" % b) for b in range(2)]
+        x_rows = [keep.tile([P, LOW_ROWS * SIDE], BF16, name="x_rows%d" % b) for b in range(2)]
+        x_top = [keep.tile([P, TOP_ROWS, TOP_PITCH], BF16, name="x_top%d" % b) for b in range(2)]
         nc.vector.memset(x_rows[0][:], 0.0)
+        nc.vector.memset(x_top[0][:], 0.0)
         warm = keep.tile([P, 2, 8], BF16)
         nc.gpsimd.memset(warm[:, 0, :], 0.0)
         nc.scalar.copy(out=warm[:, 1, :], in_=warm[:, 0, :])
         nc.gpsimd.memset(x_rows[1][:], 0.0)
+        nc.gpsimd.memset(x_top[1][:], 0.0)
         w_planes = keep.tile([P, PASSES, OUT_CH], U8, align_bytes=64)
         nc.vector.memset(w_planes[:].bitcast(I32), 0)
 
@@ -66,12 +70,19 @@ def tile_fast2order_de_conv_kernel(tc, x, W_words, W_scales, out):
                         in_=x_flat[n, :, iw0 : iw0 + PIXELS - 1],
                     )
             for jh in range(4):
-                count = min(WIN_ROWS, SIDE - jh)
+                count = min(LOW_ROWS, SIDE - jh)
                 rows = x_flat[n, :, SIDE * jh : SIDE * (jh + count)]
                 nc.sync.dma_start(
                     out=x_rows[n % 2][jh:P:4, 0 : SIDE * count],
                     in_=rows.unsqueeze(1).to_broadcast([CHANNELS, 2, SIDE * count]),
                 )
+            for jh in range(1, 4):
+                for r in range(max(0, TOP_ROWS - jh), TOP_ROWS):
+                    row = x_flat[n, :, SIDE * (r + jh - TOP_ROWS) : SIDE * (r + jh - TOP_ROWS + 1)]
+                    nc.sync.dma_start(
+                        out=x_top[n % 2][jh:P:4, r, 0:SIDE],
+                        in_=row.unsqueeze(1).to_broadcast([CHANNELS, 2, SIDE]),
+                    )
 
         load_image(0)
 
@@ -106,44 +117,44 @@ def tile_fast2order_de_conv_kernel(tc, x, W_words, W_scales, out):
                     )
                 )
             for phase in range(PHASES):
-                pieces.append(
-                    (wins[n][:, :, GRID * phase : GRID * (phase + 1)], window_rows[:, :, phase : phase + GRID])
-                )
-            return pieces
+                columns = slice(GRID * phase, GRID * (phase + 1))
+                pieces.append((wins[n][:, TOP_ROWS:, columns], window_rows[:, :, phase : phase + GRID]))
+            for phase in range(PHASES):
+                columns = slice(GRID * phase, GRID * (phase + 1))
+                pieces.append((wins[n][:, 0:TOP_ROWS, columns], x_top[n % 2][:, :, phase : phase + GRID]))
+            return pieces[0:PHASES] + pieces[SHIFTS:] + pieces[PHASES:SHIFTS]
 
         products = {}
 
         def multiply(n, iwh):
-            ta = prods.tile([P, A_ROWS * ROW], BF16, name="ta", align_bytes=64)
-            tb = prods.tile([P, B_ROWS * ROW], BF16, name="tb", align_bytes=64)
+            ta = prods.tile([P, T_ROWS * ROW], BF16, name="ta", align_bytes=64)
+            tb = prods.tile([P, T_ROWS * ROW], BF16, name="tb", align_bytes=64)
             f = moved.tile([P, 2, IMAGE_COLS], BF16, name="f", align_bytes=64)
             shifts = slice(2 * GRID * iwh, 2 * GRID * iwh + ROW)
             nc.vector.tensor_tensor(
                 out=ta[:].rearrange("p (u e) -> p u e", e=ROW),
-                in0=held[n][:, 0:A_ROWS, shifts],
-                in1=wins[n][:, 0:A_ROWS, :],
+                in0=held[n][:, 0:T_ROWS, shifts],
+                in1=wins[n][:, TOP_ROWS : TOP_ROWS + T_ROWS, :],
                 op=mybir.AluOpType.mult,
             )
             nc.vector.tensor_tensor(
                 out=tb[:].rearrange("p (u e) -> p u e", e=ROW),
-                in0=held[n][:, 3 : 3 + B_ROWS, shifts],
-                in1=wins[n][:, 0:B_ROWS, :],
+                in0=held[n][:, 1 : 1 + T_ROWS, shifts],
+                in1=wins[n][:, 0:T_ROWS, :],
                 op=mybir.AluOpType.mult,
             )
-            for ih in (1, 2):
-                nc.vector.tensor_tensor(
-                    out=f[:, ih - 1, 0 : OWN_ROWS[ih] * ROW].rearrange("p (u e) -> p u e", e=ROW),
-                    in0=held[n][:, ih : ih + OWN_ROWS[ih], shifts],
-                    in1=wins[n][:, 0 : OWN_ROWS[ih], :],
-                    op=mybir.AluOpType.mult,
-                )
             for jh in range(1, 4):
-                nc.sync.dma_start(out=f[jh:P:4, 0, 2 * ROW :], in_=ta[jh - 1 : P : 4, 3 * ROW : (GRID + 1) * ROW])
-            nc.sync.dma_start(out=f[0:P:4, 0, 2 * ROW :], in_=tb[2:P:4, 0 : (GRID - 2) * ROW])
+                nc.sync.dma_start(out=f[jh:P:4, 0, :], in_=ta[jh - 1 : P : 4, ROW : ROW + IMAGE_COLS])
+            nc.sync.dma_start(out=f[0:P:4, 0, :], in_=tb[2:P:4, 0:IMAGE_COLS])
             for jh in range(3):
-                nc.sync.dma_start(out=f[jh:P:4, 1, ROW:], in_=tb[jh + 1 : P : 4, 0 : (GRID - 1) * ROW])
-            nc.sync.dma_start(out=f[3:P:4, 1, ROW:], in_=ta[1:P:4, 3 * ROW : (GRID + 2) * ROW])
-            products[(n, iwh)] = {0: ta[:, 0:IMAGE_COLS], 1: f[:, 0, :], 2: f[:, 1, :], 3: tb[:]}
+                nc.sync.dma_start(out=f[jh:P:4, 1, :], in_=tb[jh + 1 : P : 4, ROW : ROW + IMAGE_COLS])
+            nc.sync.dma_start(out=f[3:P:4, 1, :], in_=ta[1:P:4, 2 * ROW : 2 * ROW + IMAGE_COLS])
+            products[(n, iwh)] = {
+                0: ta[:, 0:IMAGE_COLS],
+                1: f[:, 0, :],
+                2: f[:, 1, :],
+                3: tb[:, 2 * ROW : 2 * ROW + IMAGE_COLS],
+            }
 
         sums = {}
         done = {}
@@ -191,9 +202,9 @@ def tile_fast2order_de_conv_kernel(tc, x, W_words, W_scales, out):
         both = list(range(HALVES))
 
         first_pieces = table_pieces(0)
-        for destination, source in first_pieces[3:PHASES] + first_pieces[SHIFTS:]:
+        for destination, source in first_pieces[3 : PHASES + 2 * PHASES]:
             nc.vector.tensor_copy(out=destination, in_=source)
-        for destination, source in first_pieces[0:3] + first_pieces[PHASES:SHIFTS]:
+        for destination, source in first_pieces[0:3] + first_pieces[PHASES + 2 * PHASES :]:
             nc.scalar.copy(out=destination, in_=source)
         for destination, source in table_pieces(1):
             nc.scalar.copy(out=destination, in_=source)

@@ -43,7 +43,7 @@ def tile_fast2order_de_conv_kernel(tc, x, W_words, W_scales, out):
         keep = ctx.enter_context(tc.tile_pool(name="keep", bufs=1))
         tables = ctx.enter_context(tc.tile_pool(name="tables", bufs=2))
         prods = ctx.enter_context(tc.tile_pool(name="prods", bufs=3))
-        moved = ctx.enter_context(tc.tile_pool(name="moved", bufs=3))
+        moved = ctx.enter_context(tc.tile_pool(name="moved", bufs=4))
         packed = ctx.enter_context(tc.tile_pool(name="packed", bufs=4))
         results = ctx.enter_context(tc.tile_pool(name="results", bufs=4))
         psum = ctx.enter_context(tc.psum_pool(name="psum", bufs=2))
@@ -225,10 +225,10 @@ def tile_fast2order_de_conv_kernel(tc, x, W_words, W_scales, out):
                 load_image(n + 3)
             if not last:
                 multiply(n + 1, 0)
+                multiply(n + 1, 1)
             contract(n, 1, 0, both)
             contract(n, 2, 0, both)
             if not last:
-                multiply(n + 1, 1)
                 contract(n, 1, 1, both)
                 contract(n, 2, 1, both)
                 for half in both:

@@ -102,47 +102,52 @@ def tile_fast2order_de_conv_kernel(tc, x, W_words, W_scales, out):
         held = {}
         wins = {}
 
-        def table_pieces(n):
+        def table_pieces(n, cuts):
             held[n] = tables.tile([P, SIDE, SHIFTS * GRID], BF16, name="held")
             wins[n] = tables.tile([P, WIN_ROWS, ROW], BF16, name="wins")
             image_rows = x_held[n % 2][:].rearrange("p (h w) -> p h w", w=SIDE)
             window_rows = x_rows[n % 2][:].rearrange("p (r w) -> p r w", w=SIDE)
-            pieces = []
-            for shift in range(SHIFTS):
-                every_fourth = image_rows[:, :, shift : shift + PACK * (QUADS - 1) + 1 : PACK]
-                pieces.append(
-                    (
-                        held[n][:, :, GRID * shift : GRID * (shift + 1)].rearrange("p h (q t) -> p h q t", t=PACK),
-                        every_fourth.unsqueeze(3).to_broadcast([P, SIDE, QUADS, PACK]),
-                    )
+
+            def shift_piece(shift, first, last):
+                every_fourth = image_rows[:, first:last, shift : shift + PACK * (QUADS - 1) + 1 : PACK]
+                return (
+                    held[n][:, first:last, GRID * shift : GRID * (shift + 1)].rearrange("p h (q t) -> p h q t", t=PACK),
+                    every_fourth.unsqueeze(3).to_broadcast([P, last - first, QUADS, PACK]),
                 )
+
+            early = [shift_piece(shift, first, last) for first, last in cuts for shift in range(PHASES)]
+            late = [shift_piece(shift, 0, SIDE) for shift in range(PHASES, SHIFTS)]
+            pieces = []
             for phase in range(PHASES):
                 columns = slice(GRID * phase, GRID * (phase + 1))
                 pieces.append((wins[n][:, TOP_ROWS:, columns], window_rows[:, :, phase : phase + GRID]))
             for phase in range(PHASES):
                 columns = slice(GRID * phase, GRID * (phase + 1))
                 pieces.append((wins[n][:, 0:TOP_ROWS, columns], x_top[n % 2][:, :, phase : phase + GRID]))
-            return pieces[0:PHASES] + pieces[SHIFTS:] + pieces[PHASES:SHIFTS]
+            return early, pieces, late
 
         products = {}
 
-        def multiply(n, iwh):
+        def multiply(n, iwh, cuts):
             ta = prods.tile([P, T_ROWS * ROW], BF16, name="ta", align_bytes=64)
             tb = prods.tile([P, T_ROWS * ROW], BF16, name="tb", align_bytes=64)
             f = moved.tile([P, 2, IMAGE_COLS], BF16, name="f", align_bytes=64)
             shifts = slice(2 * GRID * iwh, 2 * GRID * iwh + ROW)
-            nc.vector.tensor_tensor(
-                out=ta[:].rearrange("p (u e) -> p u e", e=ROW),
-                in0=held[n][:, 0:T_ROWS, shifts],
-                in1=wins[n][:, TOP_ROWS : TOP_ROWS + T_ROWS, :],
-                op=mybir.AluOpType.mult,
-            )
-            nc.vector.tensor_tensor(
-                out=tb[:].rearrange("p (u e) -> p u e", e=ROW),
-                in0=held[n][:, 1 : 1 + T_ROWS, shifts],
-                in1=wins[n][:, 0:T_ROWS, :],
-                op=mybir.AluOpType.mult,
-            )
+            for first, last in cuts:
+                a_rows = (first, min(last, T_ROWS))
+                b_rows = (max(first - 1, 0), last - 1)
+                nc.vector.tensor_tensor(
+                    out=ta[:, ROW * a_rows[0] : ROW * a_rows[1]].rearrange("p (u e) -> p u e", e=ROW),
+                    in0=held[n][:, a_rows[0] : a_rows[1], shifts],
+                    in1=wins[n][:, TOP_ROWS + a_rows[0] : TOP_ROWS + a_rows[1], :],
+                    op=mybir.AluOpType.mult,
+                )
+                nc.vector.tensor_tensor(
+                    out=tb[:, ROW * b_rows[0] : ROW * b_rows[1]].rearrange("p (u e) -> p u e", e=ROW),
+                    in0=held[n][:, 1 + b_rows[0] : 1 + b_rows[1], shifts],
+                    in1=wins[n][:, b_rows[0] : b_rows[1], :],
+                    op=mybir.AluOpType.mult,
+                )
             for jh in range(1, 4):
                 nc.sync.dma_start(out=f[jh:P:4, 0, :], in_=ta[jh - 1 : P : 4, ROW : ROW + IMAGE_COLS])
             nc.sync.dma_start(out=f[0:P:4, 0, :], in_=tb[2:P:4, 0:IMAGE_COLS])
@@ -201,16 +206,23 @@ def tile_fast2order_de_conv_kernel(tc, x, W_words, W_scales, out):
 
         both = list(range(HALVES))
 
-        first_pieces = table_pieces(0)
-        for destination, source in first_pieces[3 : PHASES + 2 * PHASES]:
-            nc.vector.tensor_copy(out=destination, in_=source)
-        for destination, source in first_pieces[0:3] + first_pieces[PHASES + 2 * PHASES :]:
-            nc.scalar.copy(out=destination, in_=source)
-        for destination, source in table_pieces(1):
-            nc.scalar.copy(out=destination, in_=source)
+        whole = [(0, SIDE)]
+        two_steps = [(0, SIDE // 2 + 1), (SIDE // 2 + 1, SIDE)]
 
-        multiply(0, 0)
-        multiply(0, 1)
+        def build_on_scalar(n):
+            early, windows, late = table_pieces(n, whole)
+            for destination, source in early + windows + late:
+                nc.scalar.copy(out=destination, in_=source)
+
+        early, windows, late = table_pieces(0, two_steps)
+        for destination, source in windows:
+            nc.vector.tensor_copy(out=destination, in_=source)
+        for destination, source in early + late:
+            nc.scalar.copy(out=destination, in_=source)
+        build_on_scalar(1)
+
+        multiply(0, 0, two_steps)
+        multiply(0, 1, whole)
         load_image(2)
         for iwh in range(2):
             contract(0, 0, iwh, both)
@@ -219,13 +231,12 @@ def tile_fast2order_de_conv_kernel(tc, x, W_words, W_scales, out):
         for n in range(IMAGES):
             last = n + 1 == IMAGES
             if n + 2 < IMAGES:
-                for destination, source in table_pieces(n + 2):
-                    nc.scalar.copy(out=destination, in_=source)
+                build_on_scalar(n + 2)
             if n + 3 < IMAGES:
                 load_image(n + 3)
             if not last:
-                multiply(n + 1, 0)
-                multiply(n + 1, 1)
+                multiply(n + 1, 0, whole)
+                multiply(n + 1, 1, whole)
             contract(n, 1, 0, both)
             contract(n, 2, 0, both)
             if not last:

@@ -33,6 +33,7 @@ TOP_ROWS = 2
 TOP_PITCH = 48
 LOW_ROWS = T_ROWS
 WIN_ROWS = TOP_ROWS + LOW_ROWS
+WARM_UPS = 6
 FLOPS = 2 * IMAGES * GRID * GRID * CHANNELS * 256 * OUT_CH
 
 
@@ -164,6 +165,18 @@ def tile_fast2order_de_conv_kernel(tc, x, W_words, W_scales, out):
         sums = {}
         done = {}
 
+        def warm_tensor(n):
+            sums[(n, 0, 0)] = psum.tile([P, N_TILE], F32, name="sums00")
+            done[(n, 0, 0)] = 0
+            for repeat in range(WARM_UPS):
+                nc.tensor.matmul(
+                    out=sums[(n, 0, 0)][:],
+                    lhsT=wins[n][:, 0, :],
+                    rhs=products[(n, 1)][0][:, 0:N_TILE],
+                    start=True,
+                    stop=True,
+                )
+
         def contract(n, ih, iwh, halves):
             a = 2 * ih + iwh
             width = len(halves) * N_TILE
@@ -223,6 +236,7 @@ def tile_fast2order_de_conv_kernel(tc, x, W_words, W_scales, out):
 
         multiply(0, 0, two_steps)
         multiply(0, 1, whole)
+        warm_tensor(0)
         load_image(2)
         for iwh in range(2):
             contract(0, 0, iwh, both)
@@ -237,6 +251,7 @@ def tile_fast2order_de_conv_kernel(tc, x, W_words, W_scales, out):
             if not last:
                 multiply(n + 1, 0, whole)
                 multiply(n + 1, 1, whole)
+                warm_tensor(n + 1)
             contract(n, 1, 0, both)
             contract(n, 2, 0, both)
             if not last:

@@ -20,7 +20,7 @@ GRID = 32
 QUADS = GRID // PACK
 PHASES = PACK
 PASSES = 8
-SHIFTS = PHASES + 2
+PAIR = 2
 TILE_ROWS = 16
 N_TILE = TILE_ROWS * GRID
 HALVES = GRID // TILE_ROWS
@@ -43,8 +43,7 @@ def tile_fast2order_de_conv_kernel(tc, x, W_words, W_scales, out):
         ctx.enter_context(tc.manual_schedule())
         keep = ctx.enter_context(tc.tile_pool(name="keep", bufs=1))
         tables = ctx.enter_context(tc.tile_pool(name="tables", bufs=2))
-        prods = ctx.enter_context(tc.tile_pool(name="prods", bufs=3))
-        moved = ctx.enter_context(tc.tile_pool(name="moved", bufs=4))
+        prods = ctx.enter_context(tc.tile_pool(name="prods", bufs=4))
         packed = ctx.enter_context(tc.tile_pool(name="packed", bufs=4))
         results = ctx.enter_context(tc.tile_pool(name="results", bufs=4))
         psum = ctx.enter_context(tc.psum_pool(name="psum", bufs=2))
@@ -95,29 +94,36 @@ def tile_fast2order_de_conv_kernel(tc, x, W_words, W_scales, out):
             )
         w_words = keep.tile([P, PASSES, 2 * OUT_CH], U8, align_bytes=64)
         words_by_pass = W_words.rearrange("g (c2 a r) b -> a (g c2) r b", c2=2, a=PASSES)
-        for a in range(PASSES):
+        words_by_jh = W_words.rearrange("g (c2 a i j) b -> a j (g c2) i b", c2=2, a=PASSES, i=2)
+        for a in (0, 1, 6, 7):
             nc.sync.dma_start(out=w_words[:, a, :].bitcast(I32), in_=words_by_pass[a].bitcast(I32))
 
         load_image(1)
+
+        for a in range(2, 6):
+            for slot in range(4):
+                jh = (slot + 1) % 4 if a // 2 == 1 else (slot + 3) % 4
+                nc.sync.dma_start(out=w_words[slot:P:4, a, :].bitcast(I32), in_=words_by_jh[a, jh].bitcast(I32))
 
         held = {}
         wins = {}
 
         def table_pieces(n, cuts):
-            held[n] = tables.tile([P, SIDE, SHIFTS * GRID], BF16, name="held")
+            held[n] = tables.tile([P, 2, SIDE, PHASES, QUADS, PAIR], BF16, name="held")
             wins[n] = tables.tile([P, WIN_ROWS, ROW], BF16, name="wins")
             image_rows = x_held[n % 2][:].rearrange("p (h w) -> p h w", w=SIDE)
             window_rows = x_rows[n % 2][:].rearrange("p (r w) -> p r w", w=SIDE)
 
-            def shift_piece(shift, first, last):
+            def shift_piece(iwh, phase, first, last):
+                shift = 2 * iwh + phase
                 every_fourth = image_rows[:, first:last, shift : shift + PACK * (QUADS - 1) + 1 : PACK]
                 return (
-                    held[n][:, first:last, GRID * shift : GRID * (shift + 1)].rearrange("p h (q t) -> p h q t", t=PACK),
-                    every_fourth.unsqueeze(3).to_broadcast([P, last - first, QUADS, PACK]),
+                    held[n][:, iwh, first:last, phase, :, :],
+                    every_fourth.unsqueeze(3).to_broadcast([P, last - first, QUADS, PAIR]),
                 )
 
-            early = [shift_piece(shift, first, last) for first, last in cuts for shift in range(PHASES)]
-            late = [shift_piece(shift, 0, SIDE) for shift in range(PHASES, SHIFTS)]
+            early = [shift_piece(0, phase, first, last) for first, last in cuts for phase in range(PHASES)]
+            late = [shift_piece(1, phase, 0, SIDE) for phase in range(PHASES)]
             pieces = []
             for phase in range(PHASES):
                 columns = slice(GRID * phase, GRID * (phase + 1))
@@ -128,39 +134,49 @@ def tile_fast2order_de_conv_kernel(tc, x, W_words, W_scales, out):
             return early, pieces, late
 
         products = {}
+        pairs = {}
 
         def multiply(n, iwh, cuts):
             ta = prods.tile([P, T_ROWS * ROW], BF16, name="ta", align_bytes=64)
             tb = prods.tile([P, T_ROWS * ROW], BF16, name="tb", align_bytes=64)
-            f = moved.tile([P, 2, IMAGE_COLS], BF16, name="f", align_bytes=64)
-            shifts = slice(2 * GRID * iwh, 2 * GRID * iwh + ROW)
+
+            def pairs_of(table, first, last):
+                rows = table[:, ROW * first : ROW * last]
+                return rows.rearrange("p (w r t) -> p w r t", r=PACK // PAIR, t=PAIR)
+
+            def held_twice(first, last):
+                words = (last - first) * GRID
+                rows = held[n][:, iwh, first:last, :, :, :].rearrange("p u f q t -> p (u f q) t")
+                return rows.unsqueeze(2).to_broadcast([P, words, PACK // PAIR, PAIR])
+
+            windows = wins[n][:].rearrange("p r e -> p (r e)")
             for first, last in cuts:
                 a_rows = (first, min(last, T_ROWS))
                 b_rows = (max(first - 1, 0), last - 1)
                 nc.vector.tensor_tensor(
-                    out=ta[:, ROW * a_rows[0] : ROW * a_rows[1]].rearrange("p (u e) -> p u e", e=ROW),
-                    in0=held[n][:, a_rows[0] : a_rows[1], shifts],
-                    in1=wins[n][:, TOP_ROWS + a_rows[0] : TOP_ROWS + a_rows[1], :],
+                    out=pairs_of(ta, a_rows[0], a_rows[1]),
+                    in0=held_twice(a_rows[0], a_rows[1]),
+                    in1=pairs_of(windows, TOP_ROWS + a_rows[0], TOP_ROWS + a_rows[1]),
                     op=mybir.AluOpType.mult,
                 )
                 nc.vector.tensor_tensor(
-                    out=tb[:, ROW * b_rows[0] : ROW * b_rows[1]].rearrange("p (u e) -> p u e", e=ROW),
-                    in0=held[n][:, 1 + b_rows[0] : 1 + b_rows[1], shifts],
-                    in1=wins[n][:, b_rows[0] : b_rows[1], :],
+                    out=pairs_of(tb, b_rows[0], b_rows[1]),
+                    in0=held_twice(1 + b_rows[0], 1 + b_rows[1]),
+                    in1=pairs_of(windows, b_rows[0], b_rows[1]),
                     op=mybir.AluOpType.mult,
                 )
-            for jh in range(1, 4):
-                nc.sync.dma_start(out=f[jh:P:4, 0, :], in_=ta[jh - 1 : P : 4, ROW : ROW + IMAGE_COLS])
-            nc.sync.dma_start(out=f[0:P:4, 0, :], in_=tb[2:P:4, 0:IMAGE_COLS])
-            for jh in range(3):
-                nc.sync.dma_start(out=f[jh:P:4, 1, :], in_=tb[jh + 1 : P : 4, ROW : ROW + IMAGE_COLS])
-            nc.sync.dma_start(out=f[3:P:4, 1, :], in_=ta[1:P:4, 2 * ROW : 2 * ROW + IMAGE_COLS])
             products[(n, iwh)] = {
                 0: ta[:, 0:IMAGE_COLS],
-                1: f[:, 0, :],
-                2: f[:, 1, :],
+                1: ta[:, ROW : ROW + IMAGE_COLS],
+                2: tb[:, ROW : ROW + IMAGE_COLS],
                 3: tb[:, 2 * ROW : 2 * ROW + IMAGE_COLS],
             }
+            pairs[(n, iwh)] = (ta, tb)
+
+        def move(n, iwh):
+            ta, tb = pairs[(n, iwh)]
+            nc.sync.dma_start(out=ta[3:P:4, ROW : ROW + IMAGE_COLS], in_=tb[2:P:4, 0:IMAGE_COLS])
+            nc.sync.dma_start(out=tb[0:P:4, ROW : ROW + IMAGE_COLS], in_=ta[1:P:4, 2 * ROW : 2 * ROW + IMAGE_COLS])
 
         sums = {}
         done = {}
@@ -241,6 +257,7 @@ def tile_fast2order_de_conv_kernel(tc, x, W_words, W_scales, out):
         for iwh in range(2):
             contract(0, 0, iwh, both)
             contract(0, 3, iwh, both)
+            move(0, iwh)
 
         for n in range(IMAGES):
             last = n + 1 == IMAGES
@@ -252,6 +269,10 @@ def tile_fast2order_de_conv_kernel(tc, x, W_words, W_scales, out):
                 multiply(n + 1, 0, whole)
                 multiply(n + 1, 1, whole)
                 warm_tensor(n + 1)
+                for iwh in range(2):
+                    contract(n + 1, 0, iwh, both)
+                    contract(n + 1, 3, iwh, both)
+                    move(n + 1, iwh)
             contract(n, 1, 0, both)
             contract(n, 2, 0, both)
             if not last:
@@ -259,9 +280,6 @@ def tile_fast2order_de_conv_kernel(tc, x, W_words, W_scales, out):
                 contract(n, 2, 1, both)
                 for half in both:
                     empty(n, half, [nc.scalar.copy])
-                for iwh in range(2):
-                    contract(n + 1, 0, iwh, both)
-                    contract(n + 1, 3, iwh, both)
             else:
                 contract(n, 1, 1, [0])
                 contract(n, 2, 1, [0])

@@ -12,7 +12,10 @@ FP4X4 = mybir.dt.float4_e2m1fn_x4
 
 P = 128
 PACK = 4
+PAIR = 2
 IMAGES = 4
+SPREAD = IMAGES - 1
+SLOTS = 4
 CHANNELS = 16
 SIDE = 35
 PIXELS = SIDE * SIDE
@@ -20,7 +23,6 @@ GRID = 32
 QUADS = GRID // PACK
 PHASES = PACK
 PASSES = 8
-PAIR = 2
 TILE_ROWS = 16
 N_TILE = TILE_ROWS * GRID
 HALVES = GRID // TILE_ROWS
@@ -29,10 +31,9 @@ M_TILES = OUT_CH // P
 ROW = GRID * PACK
 IMAGE_COLS = GRID * ROW
 T_ROWS = GRID + 2
-TOP_ROWS = 2
-TOP_PITCH = 48
-LOW_ROWS = T_ROWS
-WIN_ROWS = TOP_ROWS + LOW_ROWS
+TOP_ROWS = 3
+WIN_ROWS = TOP_ROWS + T_ROWS
+RAW = WIN_ROWS * SIDE + 1
 WARM_UPS = 6
 FLOPS = 2 * IMAGES * GRID * GRID * CHANNELS * 256 * OUT_CH
 
@@ -50,41 +51,56 @@ def tile_fast2order_de_conv_kernel(tc, x, W_words, W_scales, out):
 
         x_flat = x.rearrange("n c h w -> n c (h w)")
         x_held = [keep.tile([P, PIXELS], BF16, name="x_held%d" % b) for b in range(2)]
-        x_rows = [keep.tile([P, LOW_ROWS * SIDE], BF16, name="x_rows%d" % b) for b in range(2)]
-        x_top = [keep.tile([P, TOP_ROWS, TOP_PITCH], BF16, name="x_top%d" % b) for b in range(2)]
-        nc.vector.memset(x_rows[0][:], 0.0)
-        nc.vector.memset(x_top[0][:], 0.0)
+        x_rows = [keep.tile([P, RAW], BF16, name="x_rows%d" % b) for b in range(2)]
+        x_second = [keep.tile([P, SIDE + 1], BF16, name="x_second%d" % b) for b in range(2)]
         warm = keep.tile([P, 2, 8], BF16)
-        nc.gpsimd.memset(warm[:, 0, :], 0.0)
-        nc.scalar.copy(out=warm[:, 1, :], in_=warm[:, 0, :])
-        nc.gpsimd.memset(x_rows[1][:], 0.0)
-        nc.gpsimd.memset(x_top[1][:], 0.0)
+        for b, engine in enumerate([nc.vector, nc.gpsimd]):
+            engine.memset(x_rows[b][:, 0 : 2 * SIDE + 2], 0.0)
+            engine.memset(x_rows[b][:, 35 * SIDE - 1 :], 0.0)
+            engine.memset(x_second[b][:], 0.0)
+            if b == 0:
+                nc.gpsimd.memset(warm[:, 0, :], 0.0)
+                nc.scalar.copy(out=warm[:, 1, :], in_=warm[:, 0, :])
         w_planes = keep.tile([P, PASSES, OUT_CH], U8, align_bytes=64)
         nc.vector.memset(w_planes[:].bitcast(I32), 0)
 
-        def load_image(n):
+        def load_held(b, images):
             for iw0 in range(2):
-                for jh in range(4):
+                for slot in range(SLOTS):
                     nc.sync.dma_start(
-                        out=x_held[n % 2][4 * iw0 + jh : P : 8, 0 : PIXELS - 1],
-                        in_=x_flat[n, :, iw0 : iw0 + PIXELS - 1],
+                        out=x_held[b][4 * iw0 + slot : P : 8, 0 : PIXELS - 1],
+                        in_=x_flat[images[slot], :, iw0 : iw0 + PIXELS - 1],
                     )
-            for jh in range(4):
-                count = min(LOW_ROWS, SIDE - jh)
-                rows = x_flat[n, :, SIDE * jh : SIDE * (jh + count)]
-                nc.sync.dma_start(
-                    out=x_rows[n % 2][jh:P:4, 0 : SIDE * count],
-                    in_=rows.unsqueeze(1).to_broadcast([CHANNELS, 2, SIDE * count]),
-                )
-            for jh in range(1, 4):
-                for r in range(max(0, TOP_ROWS - jh), TOP_ROWS):
-                    row = x_flat[n, :, SIDE * (r + jh - TOP_ROWS) : SIDE * (r + jh - TOP_ROWS + 1)]
+
+        def load_rows(b, slot, image, place, first, count):
+            rows = x_flat[image, :, SIDE * first : SIDE * (first + count)]
+            nc.sync.dma_start(
+                out=x_rows[b][slot:P:SLOTS, SIDE * place : SIDE * (place + count)],
+                in_=rows.unsqueeze(1).to_broadcast([CHANNELS, 2, SIDE * count]),
+            )
+
+        def load_pair(n, b):
+            images = [SPREAD] + [n] * (SLOTS - 1)
+            below = [n + 1] + list(range(1, SLOTS))
+            load_held(b, images)
+            for slot in range(SLOTS):
+                place = 0 if below[slot] == 3 else 2
+                first = place + below[slot] - TOP_ROWS
+                load_rows(b, slot, images[slot], place, first, min(WIN_ROWS - place, SIDE - first))
+            for slot in range(SLOTS):
+                if below[slot] > 1:
+                    row = x_flat[images[slot], :, SIDE * (below[slot] - 2) : SIDE * (below[slot] - 1)]
                     nc.sync.dma_start(
-                        out=x_top[n % 2][jh:P:4, r, 0:SIDE],
+                        out=x_second[b][slot:P:SLOTS, 0:SIDE],
                         in_=row.unsqueeze(1).to_broadcast([CHANNELS, 2, SIDE]),
                     )
 
-        load_image(0)
+        def load_squares(b):
+            load_held(b, list(range(SLOTS)))
+            for slot in range(SLOTS):
+                load_rows(b, slot, slot, 0, 0, SIDE)
+
+        load_pair(0, 0)
 
         scale_rows = W_scales.rearrange("g (c2 a) o -> (g c2) (a o)", c2=2)
         for quadrant in range(4):
@@ -95,113 +111,112 @@ def tile_fast2order_de_conv_kernel(tc, x, W_words, W_scales, out):
         w_words = keep.tile([P, PASSES, 2 * OUT_CH], U8, align_bytes=64)
         words_by_pass = W_words.rearrange("g (c2 a r) b -> a (g c2) r b", c2=2, a=PASSES)
         words_by_jh = W_words.rearrange("g (c2 a i j) b -> a j (g c2) i b", c2=2, a=PASSES, i=2)
-        for a in (0, 1, 6, 7):
-            nc.sync.dma_start(out=w_words[:, a, :].bitcast(I32), in_=words_by_pass[a].bitcast(I32))
 
-        load_image(1)
+        def load_words(ih):
+            for a in (2 * ih, 2 * ih + 1):
+                if ih == 0:
+                    nc.sync.dma_start(out=w_words[:, a, :].bitcast(I32), in_=words_by_pass[a].bitcast(I32))
+                else:
+                    for slot in range(SLOTS):
+                        jh = (slot + ih) % SLOTS
+                        nc.sync.dma_start(
+                            out=w_words[slot:P:SLOTS, a, :].bitcast(I32), in_=words_by_jh[a, jh].bitcast(I32)
+                        )
 
-        for a in range(2, 6):
-            for slot in range(4):
-                jh = (slot + 1) % 4 if a // 2 == 1 else (slot + 3) % 4
-                nc.sync.dma_start(out=w_words[slot:P:4, a, :].bitcast(I32), in_=words_by_jh[a, jh].bitcast(I32))
+        load_squares(1)
+        load_words(0)
+        load_words(3)
 
         held = {}
         wins = {}
 
-        def table_pieces(n, cuts):
-            held[n] = tables.tile([P, 2, SIDE, PHASES, QUADS, PAIR], BF16, name="held")
-            wins[n] = tables.tile([P, WIN_ROWS, ROW], BF16, name="wins")
-            image_rows = x_held[n % 2][:].rearrange("p (h w) -> p h w", w=SIDE)
-            window_rows = x_rows[n % 2][:].rearrange("p (r w) -> p r w", w=SIDE)
+        def table_pieces(g, b, cuts, second):
+            held[g] = tables.tile([P, 2, SIDE, PHASES, QUADS, PAIR], BF16, name="held")
+            wins[g] = tables.tile([P, WIN_ROWS, ROW], BF16, name="wins")
+            image_rows = x_held[b][:].rearrange("p (h w) -> p h w", w=SIDE)
+            window_rows = x_rows[b][:, 0 : RAW - 1].rearrange("p (r w) -> p r w", w=SIDE)
 
-            def shift_piece(iwh, phase, first, last):
+            def held_piece(iwh, phase, first, last):
                 shift = 2 * iwh + phase
                 every_fourth = image_rows[:, first:last, shift : shift + PACK * (QUADS - 1) + 1 : PACK]
                 return (
-                    held[n][:, iwh, first:last, phase, :, :],
+                    held[g][:, iwh, first:last, phase, :, :],
                     every_fourth.unsqueeze(3).to_broadcast([P, last - first, QUADS, PAIR]),
                 )
 
-            early = [shift_piece(0, phase, first, last) for first, last in cuts for phase in range(PHASES)]
-            late = [shift_piece(1, phase, 0, SIDE) for phase in range(PHASES)]
-            pieces = []
+            early = [held_piece(0, phase, first, last) for first, last in cuts for phase in range(PHASES)]
+            late = [held_piece(1, phase, 0, SIDE) for phase in range(PHASES)]
+            rows = WIN_ROWS if second else SIDE
+            windows = []
             for phase in range(PHASES):
                 columns = slice(GRID * phase, GRID * (phase + 1))
-                pieces.append((wins[n][:, TOP_ROWS:, columns], window_rows[:, :, phase : phase + GRID]))
-            for phase in range(PHASES):
-                columns = slice(GRID * phase, GRID * (phase + 1))
-                pieces.append((wins[n][:, 0:TOP_ROWS, columns], x_top[n % 2][:, :, phase : phase + GRID]))
-            return early, pieces, late
+                windows.append((wins[g][:, 0:rows, columns], window_rows[:, 0:rows, phase : phase + GRID]))
+            if second:
+                for phase in range(PHASES):
+                    columns = slice(GRID * phase, GRID * (phase + 1))
+                    windows.append((wins[g][:, 1, columns], x_second[b][:, phase : phase + GRID]))
+            return early, windows, late
 
-        products = {}
-        pairs = {}
+        def multiply_rows(table, g, iwh, first, last, held_row, window_row):
+            rows = last - first
+            pairs = held[g][:, iwh, held_row + first : held_row + last, :, :, :].rearrange("p u f q t -> p (u f q) t")
+            words = wins[g][:, window_row + first : window_row + last, :].rearrange("p u e -> p (u e)")
+            nc.vector.tensor_tensor(
+                out=table[:, ROW * first : ROW * last].rearrange("p (w r t) -> p w r t", r=PACK // PAIR, t=PAIR),
+                in0=pairs.unsqueeze(2).to_broadcast([P, rows * GRID, PACK // PAIR, PAIR]),
+                in1=words.rearrange("p (w r t) -> p w r t", r=PACK // PAIR, t=PAIR),
+                op=mybir.AluOpType.mult,
+            )
 
-        def multiply(n, iwh, cuts):
-            ta = prods.tile([P, T_ROWS * ROW], BF16, name="ta", align_bytes=64)
-            tb = prods.tile([P, T_ROWS * ROW], BF16, name="tb", align_bytes=64)
+        ta = {}
+        tb = {}
+        squares = {}
+        for iwh in range(2):
+            ta[(SPREAD, iwh)] = keep.tile([P, T_ROWS * ROW], BF16, name="ta_spread%d" % iwh, align_bytes=64)
+            tb[(SPREAD, iwh)] = keep.tile([P, T_ROWS * ROW], BF16, name="tb_spread%d" % iwh, align_bytes=64)
+            squares[iwh] = keep.tile([P, SIDE * ROW], BF16, name="squares%d" % iwh, align_bytes=64)
 
-            def pairs_of(table, first, last):
-                rows = table[:, ROW * first : ROW * last]
-                return rows.rearrange("p (w r t) -> p w r t", r=PACK // PAIR, t=PAIR)
-
-            def held_twice(first, last):
-                words = (last - first) * GRID
-                rows = held[n][:, iwh, first:last, :, :, :].rearrange("p u f q t -> p (u f q) t")
-                return rows.unsqueeze(2).to_broadcast([P, words, PACK // PAIR, PAIR])
-
-            windows = wins[n][:].rearrange("p r e -> p (r e)")
+        def multiply_pair(n, g, iwh, cuts):
+            ta[(n, iwh)] = prods.tile([P, T_ROWS * ROW], BF16, name="ta", align_bytes=64)
+            tb[(n, iwh)] = prods.tile([P, T_ROWS * ROW], BF16, name="tb", align_bytes=64)
             for first, last in cuts:
-                a_rows = (first, min(last, T_ROWS))
-                b_rows = (max(first - 1, 0), last - 1)
-                nc.vector.tensor_tensor(
-                    out=pairs_of(ta, a_rows[0], a_rows[1]),
-                    in0=held_twice(a_rows[0], a_rows[1]),
-                    in1=pairs_of(windows, TOP_ROWS + a_rows[0], TOP_ROWS + a_rows[1]),
-                    op=mybir.AluOpType.mult,
-                )
-                nc.vector.tensor_tensor(
-                    out=pairs_of(tb, b_rows[0], b_rows[1]),
-                    in0=held_twice(1 + b_rows[0], 1 + b_rows[1]),
-                    in1=pairs_of(windows, b_rows[0], b_rows[1]),
-                    op=mybir.AluOpType.mult,
-                )
-            products[(n, iwh)] = {
-                0: ta[:, 0:IMAGE_COLS],
-                1: ta[:, ROW : ROW + IMAGE_COLS],
-                2: tb[:, ROW : ROW + IMAGE_COLS],
-                3: tb[:, 2 * ROW : 2 * ROW + IMAGE_COLS],
-            }
-            pairs[(n, iwh)] = (ta, tb)
+                multiply_rows(ta[(n, iwh)], g, iwh, first, min(last, T_ROWS), 0, TOP_ROWS)
+                multiply_rows(tb[(n, iwh)], g, iwh, max(first - 1, 0), last - 1, 1, 0)
+            for table in (ta, tb):
+                nc.sync.dma_start(out=table[(SPREAD, iwh)][n + 1 : P : SLOTS, :], in_=table[(n, iwh)][0:P:SLOTS, :])
 
-        def move(n, iwh):
-            ta, tb = pairs[(n, iwh)]
-            nc.sync.dma_start(out=ta[3:P:4, ROW : ROW + IMAGE_COLS], in_=tb[2:P:4, 0:IMAGE_COLS])
-            nc.sync.dma_start(out=tb[0:P:4, ROW : ROW + IMAGE_COLS], in_=ta[1:P:4, 2 * ROW : 2 * ROW + IMAGE_COLS])
+        def place_squares(n, iwh):
+            rows = T_ROWS - 1
+            source = squares[iwh][n:P:SLOTS, :]
+            nc.sync.dma_start(out=ta[(n, iwh)][0:P:SLOTS, 0 : ROW * rows], in_=source[:, 0 : ROW * rows])
+            nc.sync.dma_start(out=tb[(n, iwh)][0:P:SLOTS, ROW : ROW * (rows + 1)], in_=source[:, 2 * ROW : ROW * (rows + 2)])
+
+        def exchange(n, iwh):
+            a, b = ta[(n, iwh)], tb[(n, iwh)]
+            nc.sync.dma_start(out=a[3:P:SLOTS, ROW : ROW + IMAGE_COLS], in_=b[3:P:SLOTS, 0:IMAGE_COLS])
+            nc.sync.dma_start(out=b[1:P:SLOTS, ROW : ROW + IMAGE_COLS], in_=a[1:P:SLOTS, 2 * ROW : 2 * ROW + IMAGE_COLS])
 
         sums = {}
         done = {}
 
-        def warm_tensor(n):
+        def warm_tensor(n, table):
             sums[(n, 0, 0)] = psum.tile([P, N_TILE], F32, name="sums00")
             done[(n, 0, 0)] = 0
             for repeat in range(WARM_UPS):
                 nc.tensor.matmul(
-                    out=sums[(n, 0, 0)][:],
-                    lhsT=wins[n][:, 0, :],
-                    rhs=products[(n, 1)][0][:, 0:N_TILE],
-                    start=True,
-                    stop=True,
+                    out=sums[(n, 0, 0)][:], lhsT=table[:, 0:P], rhs=table[:, 0:N_TILE], start=True, stop=True
                 )
 
         def contract(n, ih, iwh, halves):
             a = 2 * ih + iwh
             width = len(halves) * N_TILE
+            table = (ta if ih < 2 else tb)[(n, iwh)]
+            row = (0, 1, 1, 2)[ih]
             codes = packed.tile([P, HALVES * N_TILE], U32, name="codes", align_bytes=64)
             scales = packed.tile([P, HALVES * N_TILE], U8, name="scales", align_bytes=64)
+            begin = ROW * row + PACK * N_TILE * halves[0]
             nc.vector.quantize_mx(
-                out=codes[:, 0:width].bitcast(FP8X4),
-                scales=scales[:, 0:width],
-                in_=products[(n, iwh)][ih][:, PACK * N_TILE * halves[0] : PACK * N_TILE * (halves[-1] + 1)],
+                out=codes[:, 0:width].bitcast(FP8X4), scales=scales[:, 0:width], in_=table[:, begin : begin + PACK * width]
             )
             for place, half in enumerate(halves):
                 for m in range(M_TILES):
@@ -234,56 +249,65 @@ def tile_fast2order_de_conv_kernel(tc, x, W_words, W_scales, out):
                 )
 
         both = list(range(HALVES))
-
         whole = [(0, SIDE)]
         two_steps = [(0, SIDE // 2 + 1), (SIDE // 2 + 1, SIDE)]
 
-        def build_on_scalar(n):
-            early, windows, late = table_pieces(n, whole)
+        def build_on_scalar(g, b, second):
+            early, windows, late = table_pieces(g, b, whole, second)
             for destination, source in early + windows + late:
                 nc.scalar.copy(out=destination, in_=source)
 
-        early, windows, late = table_pieces(0, two_steps)
+        def outer_passes(n):
+            for iwh in range(2):
+                contract(n, 0, iwh, both)
+                contract(n, 3, iwh, both)
+                exchange(n, iwh)
+
+        def inner_passes(n):
+            for iwh in range(2):
+                contract(n, 1, iwh, both)
+                contract(n, 2, iwh, both)
+            for half in both:
+                empty(n, half, [nc.scalar.copy])
+
+        early, windows, late = table_pieces(0, 0, two_steps, True)
         for destination, source in windows:
             nc.vector.tensor_copy(out=destination, in_=source)
         for destination, source in early + late:
             nc.scalar.copy(out=destination, in_=source)
-        build_on_scalar(1)
+        load_pair(1, 0)
+        load_words(1)
+        load_words(2)
+        multiply_pair(0, 0, 0, two_steps)
+        multiply_pair(0, 0, 1, whole)
 
-        multiply(0, 0, two_steps)
-        multiply(0, 1, whole)
-        warm_tensor(0)
-        load_image(2)
+        build_on_scalar(1, 1, False)
         for iwh in range(2):
-            contract(0, 0, iwh, both)
-            contract(0, 3, iwh, both)
-            move(0, iwh)
+            multiply_rows(squares[iwh], 1, iwh, 0, SIDE, 0, 0)
+            place_squares(0, iwh)
+            place_squares(SPREAD, iwh)
+        load_pair(2, 1)
+        warm_tensor(0, squares[0])
+        build_on_scalar(2, 0, True)
+        outer_passes(0)
 
-        for n in range(IMAGES):
-            last = n + 1 == IMAGES
-            if n + 2 < IMAGES:
-                build_on_scalar(n + 2)
-            if n + 3 < IMAGES:
-                load_image(n + 3)
-            if not last:
-                multiply(n + 1, 0, whole)
-                multiply(n + 1, 1, whole)
-                warm_tensor(n + 1)
-                for iwh in range(2):
-                    contract(n + 1, 0, iwh, both)
-                    contract(n + 1, 3, iwh, both)
-                    move(n + 1, iwh)
-            contract(n, 1, 0, both)
-            contract(n, 2, 0, both)
-            if not last:
-                contract(n, 1, 1, both)
-                contract(n, 2, 1, both)
-                for half in both:
-                    empty(n, half, [nc.scalar.copy])
-            else:
-                contract(n, 1, 1, [0])
-                contract(n, 2, 1, [0])
-                empty(n, 0, [nc.scalar.copy])
-                contract(n, 1, 1, [1])
-                contract(n, 2, 1, [1])
-                empty(n, 1, [nc.scalar.copy, nc.vector.tensor_copy])
+        for n in (1, 2):
+            for iwh in range(2):
+                multiply_pair(n, n + 1, iwh, whole)
+                place_squares(n, iwh)
+            if n == 1:
+                build_on_scalar(3, 1, True)
+            warm_tensor(n, tb[(n, 0)])
+            inner_passes(n - 1)
+            outer_passes(n)
+
+        outer_passes(SPREAD)
+        inner_passes(2)
+        contract(SPREAD, 1, 0, both)
+        contract(SPREAD, 2, 0, both)
+        contract(SPREAD, 1, 1, [0])
+        contract(SPREAD, 2, 1, [0])
+        empty(SPREAD, 0, [nc.scalar.copy])
+        contract(SPREAD, 1, 1, [1])
+        contract(SPREAD, 2, 1, [1])
+        empty(SPREAD, 1, [nc.scalar.copy, nc.vector.tensor_copy])

@@ -1,6 +1,7 @@
 from contextlib import ExitStack
 
 import concourse.mybir as mybir
+from concourse.masks import make_identity
 
 BF16 = mybir.dt.bfloat16
 F32 = mybir.dt.float32
@@ -34,6 +35,7 @@ T_ROWS = GRID + 2
 TOP_ROWS = 3
 WIN_ROWS = TOP_ROWS + T_ROWS
 RAW = WIN_ROWS * SIDE + 1
+BANK_ROWS = 14
 WARM_UPS = 6
 FLOPS = 2 * IMAGES * GRID * GRID * CHANNELS * 256 * OUT_CH
 
@@ -46,7 +48,7 @@ def tile_fast2order_de_conv_kernel(tc, x, W_words, W_scales, out):
         tables = ctx.enter_context(tc.tile_pool(name="tables", bufs=2))
         prods = ctx.enter_context(tc.tile_pool(name="prods", bufs=4))
         packed = ctx.enter_context(tc.tile_pool(name="packed", bufs=4))
-        results = ctx.enter_context(tc.tile_pool(name="results", bufs=4))
+        results = ctx.enter_context(tc.tile_pool(name="results", bufs=8))
         psum = ctx.enter_context(tc.psum_pool(name="psum", bufs=2))
 
         x_flat = x.rearrange("n c h w -> n c (h w)")
@@ -80,9 +82,12 @@ def tile_fast2order_de_conv_kernel(tc, x, W_words, W_scales, out):
             )
 
         def load_pair(n, b):
+            load_held(b, [SPREAD] + [n] * (SLOTS - 1))
+            load_windows(n, b)
+
+        def load_windows(n, b):
             images = [SPREAD] + [n] * (SLOTS - 1)
             below = [n + 1] + list(range(1, SLOTS))
-            load_held(b, images)
             for slot in range(SLOTS):
                 place = 0 if below[slot] == 3 else 2
                 first = place + below[slot] - TOP_ROWS
@@ -100,7 +105,33 @@ def tile_fast2order_de_conv_kernel(tc, x, W_words, W_scales, out):
             for slot in range(SLOTS):
                 load_rows(b, slot, slot, 0, 0, SIDE)
 
-        load_pair(0, 0)
+        x_first = keep.tile([P, PIXELS - 1], BF16)
+        for m in range(4):
+            image, iw0 = ((0, 0), (0, 1), (SPREAD, 0), (SPREAD, 1))[m]
+            piece = x_flat[image, :, iw0 : iw0 + PIXELS - 1]
+            nc.sync.dma_start(out=x_first[m:P:4, :], in_=piece.unsqueeze(1).to_broadcast([CHANNELS, 2, PIXELS - 1]))
+        load_windows(0, 0)
+        identity = keep.tile([P, P], BF16)
+        make_identity(nc, identity[:])
+        spreader = keep.tile([P, P], BF16)
+        to_slots = spreader[:].rearrange("k (c i s) -> k c i s", c=CHANNELS, s=SLOTS)
+        picks = identity[:].rearrange("k (c m) -> k c m", c=CHANNELS)
+        nc.vector.tensor_copy(out=to_slots[:, :, :, 0], in_=picks[:, :, 2:4])
+        nc.vector.tensor_copy(
+            out=to_slots[:, :, :, 1:SLOTS], in_=picks[:, :, 0:2].unsqueeze(3).to_broadcast([P, CHANNELS, 2, SLOTS - 1])
+        )
+        banks = []
+        for k, tag in enumerate(("sums00", "sums01", "sums10")):
+            columns = min(BANK_ROWS * SIDE, PIXELS - 1 - BANK_ROWS * SIDE * k)
+            bank = psum.tile([P, N_TILE], F32, name=tag)
+            nc.tensor.matmul(
+                out=bank[:, 0:columns],
+                lhsT=spreader[:],
+                rhs=x_first[:, BANK_ROWS * SIDE * k : BANK_ROWS * SIDE * k + columns],
+                start=True,
+                stop=True,
+            )
+            banks.append(bank)
 
         scale_rows = W_scales.rearrange("g (c2 a) o -> (g c2) (a o)", c2=2)
         for quadrant in range(4):
@@ -130,7 +161,7 @@ def tile_fast2order_de_conv_kernel(tc, x, W_words, W_scales, out):
         held = {}
         wins = {}
 
-        def table_pieces(g, b, cuts, second):
+        def table_pieces(g, b, second):
             held[g] = tables.tile([P, 2, SIDE, PHASES, QUADS, PAIR], BF16, name="held")
             wins[g] = tables.tile([P, WIN_ROWS, ROW], BF16, name="wins")
             image_rows = x_held[b][:].rearrange("p (h w) -> p h w", w=SIDE)
@@ -144,7 +175,7 @@ def tile_fast2order_de_conv_kernel(tc, x, W_words, W_scales, out):
                     every_fourth.unsqueeze(3).to_broadcast([P, last - first, QUADS, PAIR]),
                 )
 
-            early = [held_piece(0, phase, first, last) for first, last in cuts for phase in range(PHASES)]
+            early = [held_piece(0, phase, 0, SIDE) for phase in range(PHASES)]
             late = [held_piece(1, phase, 0, SIDE) for phase in range(PHASES)]
             rows = WIN_ROWS if second else SIDE
             windows = []
@@ -176,12 +207,16 @@ def tile_fast2order_de_conv_kernel(tc, x, W_words, W_scales, out):
             tb[(SPREAD, iwh)] = keep.tile([P, T_ROWS * ROW], BF16, name="tb_spread%d" % iwh, align_bytes=64)
             squares[iwh] = keep.tile([P, SIDE * ROW], BF16, name="squares%d" % iwh, align_bytes=64)
 
-        def multiply_pair(n, g, iwh, cuts):
+        def open_pair(n, iwh):
             ta[(n, iwh)] = prods.tile([P, T_ROWS * ROW], BF16, name="ta", align_bytes=64)
             tb[(n, iwh)] = prods.tile([P, T_ROWS * ROW], BF16, name="tb", align_bytes=64)
-            for first, last in cuts:
-                multiply_rows(ta[(n, iwh)], g, iwh, first, min(last, T_ROWS), 0, TOP_ROWS)
-                multiply_rows(tb[(n, iwh)], g, iwh, max(first - 1, 0), last - 1, 1, 0)
+
+        def multiply_pair(n, g, iwh):
+            open_pair(n, iwh)
+            multiply_rows(ta[(n, iwh)], g, iwh, 0, T_ROWS, 0, TOP_ROWS)
+            multiply_rows(tb[(n, iwh)], g, iwh, 0, T_ROWS, 1, 0)
+
+        def spread(n, iwh):
             for table in (ta, tb):
                 nc.sync.dma_start(out=table[(SPREAD, iwh)][n + 1 : P : SLOTS, :], in_=table[(n, iwh)][0:P:SLOTS, :])
 
@@ -234,14 +269,14 @@ def tile_fast2order_de_conv_kernel(tc, x, W_words, W_scales, out):
                     )
                     done[(n, half, m)] += 1
 
-        def empty(n, half, emptiers):
+        def empty(n, half, emptiers, stores):
             for m in range(M_TILES):
                 result = results.tile([P, TILE_ROWS, QUADS, PHASES], F32, name="result")
                 emptiers[m % len(emptiers)](
                     out=result[:],
                     in_=sums[(n, half, m)][:].rearrange("o (y s q) -> o y q s", s=PHASES, y=TILE_ROWS),
                 )
-                nc.sync.dma_start(
+                stores[m % len(stores)].dma_start(
                     out=out[n, P * m : P * (m + 1), TILE_ROWS * half : TILE_ROWS * (half + 1), :].rearrange(
                         "o y z -> o (y z)"
                     ),
@@ -249,65 +284,91 @@ def tile_fast2order_de_conv_kernel(tc, x, W_words, W_scales, out):
                 )
 
         both = list(range(HALVES))
-        whole = [(0, SIDE)]
-        two_steps = [(0, SIDE // 2 + 1), (SIDE // 2 + 1, SIDE)]
 
         def build_on_scalar(g, b, second):
-            early, windows, late = table_pieces(g, b, whole, second)
+            early, windows, late = table_pieces(g, b, second)
             for destination, source in early + windows + late:
                 nc.scalar.copy(out=destination, in_=source)
 
-        def outer_passes(n):
-            for iwh in range(2):
-                contract(n, 0, iwh, both)
-                contract(n, 3, iwh, both)
-                exchange(n, iwh)
+        def outer_passes(n, iwh):
+            contract(n, 0, iwh, both)
+            contract(n, 3, iwh, both)
+            exchange(n, iwh)
 
         def inner_passes(n):
             for iwh in range(2):
                 contract(n, 1, iwh, both)
                 contract(n, 2, iwh, both)
             for half in both:
-                empty(n, half, [nc.scalar.copy])
+                empty(n, half, [nc.scalar.copy], [nc.scalar])
 
-        early, windows, late = table_pieces(0, 0, two_steps, True)
-        for destination, source in windows:
+        early, windows, late = table_pieces(0, 0, True)
+        for destination, source in windows[:PHASES]:
             nc.vector.tensor_copy(out=destination, in_=source)
-        for destination, source in early + late:
-            nc.scalar.copy(out=destination, in_=source)
-        load_pair(1, 0)
-        load_words(1)
-        load_words(2)
-        multiply_pair(0, 0, 0, two_steps)
-        multiply_pair(0, 0, 1, whole)
+        for iwh in range(2):
+            for k, bank in enumerate(banks):
+                first, last = BANK_ROWS * k, min(SIDE, BANK_ROWS * (k + 1))
+                rows = bank[:, 0 : (last - first) * SIDE].rearrange("p (h w) -> p h w", w=SIDE)
+                for phase in range(PHASES):
+                    shift = 2 * iwh + phase
+                    every_fourth = rows[:, :, shift : shift + PACK * (QUADS - 1) + 1 : PACK]
+                    nc.scalar.copy(
+                        out=held[0][:, iwh, first:last, phase, :, :],
+                        in_=every_fourth.unsqueeze(3).to_broadcast([P, last - first, QUADS, PAIR]),
+                    )
+        open_pair(0, 0)
+        multiply_rows(ta[(0, 0)], 0, 0, 0, BANK_ROWS, 0, TOP_ROWS)
+        for destination, source in windows[PHASES:]:
+            nc.vector.tensor_copy(out=destination, in_=source)
+        multiply_rows(tb[(0, 0)], 0, 0, 0, BANK_ROWS - 1, 1, 0)
+        multiply_rows(ta[(0, 0)], 0, 0, BANK_ROWS, T_ROWS, 0, TOP_ROWS)
+        multiply_rows(tb[(0, 0)], 0, 0, BANK_ROWS - 1, T_ROWS, 1, 0)
+        multiply_pair(0, 0, 1)
 
+        spread(0, 0)
+        load_pair(1, 0)
+        spread(0, 1)
         build_on_scalar(1, 1, False)
         for iwh in range(2):
             multiply_rows(squares[iwh], 1, iwh, 0, SIDE, 0, 0)
             place_squares(0, iwh)
-            place_squares(SPREAD, iwh)
-        load_pair(2, 1)
         warm_tensor(0, squares[0])
         build_on_scalar(2, 0, True)
-        outer_passes(0)
+        load_pair(2, 1)
+        outer_passes(0, 0)
+        outer_passes(0, 1)
+        load_words(1)
+        load_words(2)
+        for iwh in range(2):
+            place_squares(SPREAD, iwh)
+        build_on_scalar(3, 1, True)
 
-        for n in (1, 2):
-            for iwh in range(2):
-                multiply_pair(n, n + 1, iwh, whole)
-                place_squares(n, iwh)
-            if n == 1:
-                build_on_scalar(3, 1, True)
-            warm_tensor(n, tb[(n, 0)])
-            inner_passes(n - 1)
-            outer_passes(n)
+        def streams(n, iwh, warm_up=False):
+            multiply_pair(n, n + 1, iwh)
+            if warm_up:
+                warm_tensor(n, tb[(n, iwh)])
+            spread(n, iwh)
+            place_squares(n, iwh)
 
-        outer_passes(SPREAD)
+        streams(1, 0, True)
+        streams(1, 1)
+        inner_passes(0)
+        streams(2, 0)
+        outer_passes(1, 0)
+        outer_passes(1, 1)
+        streams(2, 1)
+        inner_passes(1)
+        outer_passes(2, 0)
+        outer_passes(2, 1)
+
+        outer_passes(SPREAD, 0)
+        outer_passes(SPREAD, 1)
         inner_passes(2)
         contract(SPREAD, 1, 0, both)
         contract(SPREAD, 2, 0, both)
         contract(SPREAD, 1, 1, [0])
         contract(SPREAD, 2, 1, [0])
-        empty(SPREAD, 0, [nc.scalar.copy])
+        empty(SPREAD, 0, [nc.scalar.copy], [nc.scalar])
         contract(SPREAD, 1, 1, [1])
         contract(SPREAD, 2, 1, [1])
-        empty(SPREAD, 1, [nc.scalar.copy, nc.vector.tensor_copy])
+        empty(SPREAD, 1, [nc.scalar.copy, nc.vector.tensor_copy], [nc.scalar, nc.sync])

@@ -300,7 +300,7 @@ def tile_fast2order_de_conv_kernel(tc, x, W_words, W_scales, out):
                 contract(n, 1, iwh, both)
                 contract(n, 2, iwh, both)
             for half in both:
-                empty(n, half, [nc.scalar.copy], [nc.scalar])
+                empty(n, half, [nc.scalar.copy], [nc.sync])
 
         early, windows, late = table_pieces(0, 0, True)
         for destination, source in windows[:PHASES]:
@@ -368,7 +368,7 @@ def tile_fast2order_de_conv_kernel(tc, x, W_words, W_scales, out):
         contract(SPREAD, 2, 0, both)
         contract(SPREAD, 1, 1, [0])
         contract(SPREAD, 2, 1, [0])
-        empty(SPREAD, 0, [nc.scalar.copy], [nc.scalar])
+        empty(SPREAD, 0, [nc.scalar.copy], [nc.sync])
         contract(SPREAD, 1, 1, [1])
         contract(SPREAD, 2, 1, [1])
-        empty(SPREAD, 1, [nc.scalar.copy, nc.vector.tensor_copy], [nc.scalar, nc.sync])
+        empty(SPREAD, 1, [nc.scalar.copy, nc.vector.tensor_copy], [nc.sync])

@@ -17,6 +17,7 @@ PAIR = 2
 IMAGES = 4
 SPREAD = IMAGES - 1
 SLOTS = 4
+SQUARES = SPREAD + 1
 CHANNELS = 16
 SIDE = 35
 PIXELS = SIDE * SIDE
@@ -32,10 +33,10 @@ M_TILES = OUT_CH // P
 ROW = GRID * PACK
 IMAGE_COLS = GRID * ROW
 T_ROWS = GRID + 2
+TABLE = SIDE * ROW
 TOP_ROWS = 3
 WIN_ROWS = TOP_ROWS + T_ROWS
-RAW = WIN_ROWS * SIDE + 1
-BANK_ROWS = 14
+BANKS = [(0, 7), (7, 21), (21, 35)]
 WARM_UPS = 6
 FLOPS = 2 * IMAGES * GRID * GRID * CHANNELS * 256 * OUT_CH
 
@@ -45,92 +46,48 @@ def tile_fast2order_de_conv_kernel(tc, x, W_words, W_scales, out):
     with ExitStack() as ctx:
         ctx.enter_context(tc.manual_schedule())
         keep = ctx.enter_context(tc.tile_pool(name="keep", bufs=1))
-        tables = ctx.enter_context(tc.tile_pool(name="tables", bufs=2))
-        prods = ctx.enter_context(tc.tile_pool(name="prods", bufs=4))
+        prods = ctx.enter_context(tc.tile_pool(name="prods", bufs=2))
         packed = ctx.enter_context(tc.tile_pool(name="packed", bufs=4))
-        results = ctx.enter_context(tc.tile_pool(name="results", bufs=8))
+        outs = ctx.enter_context(tc.tile_pool(name="outs", bufs=4))
         psum = ctx.enter_context(tc.psum_pool(name="psum", bufs=2))
 
         x_flat = x.rearrange("n c h w -> n c (h w)")
-        x_held = [keep.tile([P, PIXELS], BF16, name="x_held%d" % b) for b in range(2)]
-        x_rows = [keep.tile([P, RAW], BF16, name="x_rows%d" % b) for b in range(2)]
-        x_second = [keep.tile([P, SIDE + 1], BF16, name="x_second%d" % b) for b in range(2)]
+        x_rows = keep.tile([P, PIXELS], BF16)
+        for slot in range(SLOTS):
+            nc.sync.dma_start(
+                out=x_rows[slot:P:SLOTS, :], in_=x_flat[slot].unsqueeze(1).to_broadcast([CHANNELS, 2, PIXELS])
+            )
         warm = keep.tile([P, 2, 8], BF16)
-        for b, engine in enumerate([nc.vector, nc.gpsimd]):
-            engine.memset(x_rows[b][:, 0 : 2 * SIDE + 2], 0.0)
-            engine.memset(x_rows[b][:, 35 * SIDE - 1 :], 0.0)
-            engine.memset(x_second[b][:], 0.0)
-            if b == 0:
-                nc.gpsimd.memset(warm[:, 0, :], 0.0)
-                nc.scalar.copy(out=warm[:, 1, :], in_=warm[:, 0, :])
+        nc.gpsimd.memset(warm[:, 0, :], 0.0)
+        nc.scalar.copy(out=warm[:, 1, :], in_=warm[:, 0, :])
         w_planes = keep.tile([P, PASSES, OUT_CH], U8, align_bytes=64)
         nc.vector.memset(w_planes[:].bitcast(I32), 0)
 
-        def load_held(b, images):
-            for iw0 in range(2):
-                for slot in range(SLOTS):
-                    nc.sync.dma_start(
-                        out=x_held[b][4 * iw0 + slot : P : 8, 0 : PIXELS - 1],
-                        in_=x_flat[images[slot], :, iw0 : iw0 + PIXELS - 1],
-                    )
-
-        def load_rows(b, slot, image, place, first, count):
-            rows = x_flat[image, :, SIDE * first : SIDE * (first + count)]
-            nc.sync.dma_start(
-                out=x_rows[b][slot:P:SLOTS, SIDE * place : SIDE * (place + count)],
-                in_=rows.unsqueeze(1).to_broadcast([CHANNELS, 2, SIDE * count]),
-            )
-
-        def load_pair(n, b):
-            load_held(b, [SPREAD] + [n] * (SLOTS - 1))
-            load_windows(n, b)
-
-        def load_windows(n, b):
-            images = [SPREAD] + [n] * (SLOTS - 1)
-            below = [n + 1] + list(range(1, SLOTS))
-            for slot in range(SLOTS):
-                place = 0 if below[slot] == 3 else 2
-                first = place + below[slot] - TOP_ROWS
-                load_rows(b, slot, images[slot], place, first, min(WIN_ROWS - place, SIDE - first))
-            for slot in range(SLOTS):
-                if below[slot] > 1:
-                    row = x_flat[images[slot], :, SIDE * (below[slot] - 2) : SIDE * (below[slot] - 1)]
-                    nc.sync.dma_start(
-                        out=x_second[b][slot:P:SLOTS, 0:SIDE],
-                        in_=row.unsqueeze(1).to_broadcast([CHANNELS, 2, SIDE]),
-                    )
-
-        def load_squares(b):
-            load_held(b, list(range(SLOTS)))
-            for slot in range(SLOTS):
-                load_rows(b, slot, slot, 0, 0, SIDE)
-
-        x_first = keep.tile([P, PIXELS - 1], BF16)
-        for m in range(4):
-            image, iw0 = ((0, 0), (0, 1), (SPREAD, 0), (SPREAD, 1))[m]
-            piece = x_flat[image, :, iw0 : iw0 + PIXELS - 1]
-            nc.sync.dma_start(out=x_first[m:P:4, :], in_=piece.unsqueeze(1).to_broadcast([CHANNELS, 2, PIXELS - 1]))
-        load_windows(0, 0)
         identity = keep.tile([P, P], BF16)
         make_identity(nc, identity[:])
-        spreader = keep.tile([P, P], BF16)
-        to_slots = spreader[:].rearrange("k (c i s) -> k c i s", c=CHANNELS, s=SLOTS)
-        picks = identity[:].rearrange("k (c m) -> k c m", c=CHANNELS)
-        nc.vector.tensor_copy(out=to_slots[:, :, :, 0], in_=picks[:, :, 2:4])
-        nc.vector.tensor_copy(
-            out=to_slots[:, :, :, 1:SLOTS], in_=picks[:, :, 0:2].unsqueeze(3).to_broadcast([P, CHANNELS, 2, SLOTS - 1])
-        )
         banks = []
-        for k, tag in enumerate(("sums00", "sums01", "sums10")):
-            columns = min(BANK_ROWS * SIDE, PIXELS - 1 - BANK_ROWS * SIDE * k)
-            bank = psum.tile([P, N_TILE], F32, name=tag)
-            nc.tensor.matmul(
-                out=bank[:, 0:columns],
-                lhsT=spreader[:],
-                rhs=x_first[:, BANK_ROWS * SIDE * k : BANK_ROWS * SIDE * k + columns],
-                start=True,
-                stop=True,
+        pickers = []
+        for iw0 in range(2):
+            picker = keep.tile([P, P], BF16, name="picker%d" % iw0)
+            nc.vector.memset(picker[:], 0.0)
+            by_iw0 = "k (c i s) -> k c i s"
+            nc.vector.tensor_copy(
+                out=picker[:].rearrange(by_iw0, i=2, s=SLOTS)[:, :, iw0, :],
+                in_=identity[:].rearrange(by_iw0, i=2, s=SLOTS)[:, :, iw0, :],
             )
+            pickers.append(picker)
+        for (first, last), tag in zip(BANKS, ("sums00", "sums01", "sums10")):
+            columns = min(SIDE * last, PIXELS - 1) - SIDE * first
+            bank = psum.tile([P, N_TILE], F32, name=tag)
+            for iw0 in range(2):
+                begin = SIDE * first + iw0
+                nc.tensor.matmul(
+                    out=bank[:, 0:columns],
+                    lhsT=pickers[iw0][:],
+                    rhs=x_rows[:, begin : begin + columns],
+                    start=(iw0 == 0),
+                    stop=(iw0 == 1),
+                )
             banks.append(bank)
 
         scale_rows = W_scales.rearrange("g (c2 a) o -> (g c2) (a o)", c2=2)
@@ -141,97 +98,87 @@ def tile_fast2order_de_conv_kernel(tc, x, W_words, W_scales, out):
             )
         w_words = keep.tile([P, PASSES, 2 * OUT_CH], U8, align_bytes=64)
         words_by_pass = W_words.rearrange("g (c2 a r) b -> a (g c2) r b", c2=2, a=PASSES)
-        words_by_jh = W_words.rearrange("g (c2 a i j) b -> a j (g c2) i b", c2=2, a=PASSES, i=2)
+        w_natural = keep.tile([P, PASSES, 2 * OUT_CH], U8, align_bytes=64)
 
-        def load_words(ih):
-            for a in (2 * ih, 2 * ih + 1):
-                if ih == 0:
-                    nc.sync.dma_start(out=w_words[:, a, :].bitcast(I32), in_=words_by_pass[a].bitcast(I32))
-                else:
-                    for slot in range(SLOTS):
-                        jh = (slot + ih) % SLOTS
-                        nc.sync.dma_start(
-                            out=w_words[slot:P:SLOTS, a, :].bitcast(I32), in_=words_by_jh[a, jh].bitcast(I32)
-                        )
+        def load_words(target, a):
+            nc.sync.dma_start(out=target[:, a, :].bitcast(I32), in_=words_by_pass[a].bitcast(I32))
 
-        load_squares(1)
-        load_words(0)
-        load_words(3)
+        def turn_words(ih):
+            for slot in range(SLOTS):
+                jh = (slot + ih) % SLOTS
+                two = slice(2 * ih, 2 * ih + 2)
+                nc.sync.dma_start(
+                    out=w_words[slot:P:SLOTS, two, :].rearrange("p a o -> p (a o)").bitcast(I32),
+                    in_=w_natural[jh:P:SLOTS, two, :].rearrange("p a o -> p (a o)").bitcast(I32),
+                )
+
+        for a in (0, 1):
+            load_words(w_words, a)
+        for a in (6, 7, 2, 3, 4, 5):
+            load_words(w_natural, a)
 
         held = {}
         wins = {}
+        held[SQUARES] = keep.tile([P, 2, SIDE, PHASES, QUADS, PAIR], BF16, name="held_squares")
+        wins[SQUARES] = keep.tile([P, SIDE, ROW], BF16, name="wins_squares")
+        spare_held = [keep.tile([P, 2, SIDE, PHASES, QUADS, PAIR], BF16, name="held%d" % b) for b in range(2)]
+        spare_wins = [keep.tile([P, WIN_ROWS, ROW], BF16, name="wins%d" % b) for b in range(2)]
+        for b in range(2):
+            nc.gpsimd.memset(spare_wins[b][:, 0:2, :], 0.0)
+            nc.gpsimd.memset(spare_wins[b][:, SIDE:WIN_ROWS, :], 0.0)
 
-        def table_pieces(g, b, second):
-            held[g] = tables.tile([P, 2, SIDE, PHASES, QUADS, PAIR], BF16, name="held")
-            wins[g] = tables.tile([P, WIN_ROWS, ROW], BF16, name="wins")
-            image_rows = x_held[b][:].rearrange("p (h w) -> p h w", w=SIDE)
-            window_rows = x_rows[b][:, 0 : RAW - 1].rearrange("p (r w) -> p r w", w=SIDE)
-
-            def held_piece(iwh, phase, first, last):
-                shift = 2 * iwh + phase
-                every_fourth = image_rows[:, first:last, shift : shift + PACK * (QUADS - 1) + 1 : PACK]
-                return (
-                    held[g][:, iwh, first:last, phase, :, :],
-                    every_fourth.unsqueeze(3).to_broadcast([P, last - first, QUADS, PAIR]),
+        def fill_windows(n):
+            wins[n] = spare_wins[n % 2]
+            for slot in range(SLOTS):
+                place = TOP_ROWS - (slot if slot else n + 1)
+                image = n if slot else SPREAD
+                nc.sync.dma_start(
+                    out=wins[n][slot:P:SLOTS, place : place + SIDE, :], in_=wins[SQUARES][image:P:SLOTS, :, :]
                 )
 
-            early = [held_piece(0, phase, 0, SIDE) for phase in range(PHASES)]
-            late = [held_piece(1, phase, 0, SIDE) for phase in range(PHASES)]
-            rows = WIN_ROWS if second else SIDE
-            windows = []
-            for phase in range(PHASES):
-                columns = slice(GRID * phase, GRID * (phase + 1))
-                windows.append((wins[g][:, 0:rows, columns], window_rows[:, 0:rows, phase : phase + GRID]))
-            if second:
-                for phase in range(PHASES):
-                    columns = slice(GRID * phase, GRID * (phase + 1))
-                    windows.append((wins[g][:, 1, columns], x_second[b][:, phase : phase + GRID]))
-            return early, windows, late
+        def fill_held(n, pairs):
+            held[n] = spare_held[n % 2]
+            for slot in range(SLOTS):
+                image = n if slot else SPREAD
+                nc.sync.dma_start(out=held[n][slot:P:SLOTS, pairs], in_=held[SQUARES][image:P:SLOTS, pairs])
 
-        def multiply_rows(table, g, iwh, first, last, held_row, window_row):
-            rows = last - first
-            pairs = held[g][:, iwh, held_row + first : held_row + last, :, :, :].rearrange("p u f q t -> p (u f q) t")
-            words = wins[g][:, window_row + first : window_row + last, :].rearrange("p u e -> p (u e)")
+        def multiply_rows(table, g, iwh, first, last, below):
+            pairs = held[g][:, iwh, first:last, :, :, :].rearrange("p u f q t -> p (u f q) t")
+            words = wins[g][:, first + below : last + below, :].rearrange("p u e -> p (u e)")
             nc.vector.tensor_tensor(
                 out=table[:, ROW * first : ROW * last].rearrange("p (w r t) -> p w r t", r=PACK // PAIR, t=PAIR),
-                in0=pairs.unsqueeze(2).to_broadcast([P, rows * GRID, PACK // PAIR, PAIR]),
+                in0=pairs.unsqueeze(2).to_broadcast([P, (last - first) * GRID, PACK // PAIR, PAIR]),
                 in1=words.rearrange("p (w r t) -> p w r t", r=PACK // PAIR, t=PAIR),
                 op=mybir.AluOpType.mult,
             )
 
-        ta = {}
-        tb = {}
-        squares = {}
-        for iwh in range(2):
-            ta[(SPREAD, iwh)] = keep.tile([P, T_ROWS * ROW], BF16, name="ta_spread%d" % iwh, align_bytes=64)
-            tb[(SPREAD, iwh)] = keep.tile([P, T_ROWS * ROW], BF16, name="tb_spread%d" % iwh, align_bytes=64)
-            squares[iwh] = keep.tile([P, SIDE * ROW], BF16, name="squares%d" % iwh, align_bytes=64)
+        ta = {SPREAD: keep.tile([P, 2, TABLE], BF16, name="ta_spread", align_bytes=64)}
+        tb = {SPREAD: keep.tile([P, 2, TABLE], BF16, name="tb_spread", align_bytes=64)}
+        squares = keep.tile([P, 2, TABLE], BF16, align_bytes=64)
 
-        def open_pair(n, iwh):
-            ta[(n, iwh)] = prods.tile([P, T_ROWS * ROW], BF16, name="ta", align_bytes=64)
-            tb[(n, iwh)] = prods.tile([P, T_ROWS * ROW], BF16, name="tb", align_bytes=64)
+        def open_pair(n):
+            ta[n] = prods.tile([P, 2, TABLE], BF16, name="ta", align_bytes=64)
+            tb[n] = prods.tile([P, 2, TABLE], BF16, name="tb", align_bytes=64)
 
-        def multiply_pair(n, g, iwh):
-            open_pair(n, iwh)
-            multiply_rows(ta[(n, iwh)], g, iwh, 0, T_ROWS, 0, TOP_ROWS)
-            multiply_rows(tb[(n, iwh)], g, iwh, 0, T_ROWS, 1, 0)
+        def multiply_a(n, iwh):
+            multiply_rows(ta[n][:, iwh, :], n, iwh, 0, T_ROWS, TOP_ROWS)
 
-        def spread(n, iwh):
-            for table in (ta, tb):
-                nc.sync.dma_start(out=table[(SPREAD, iwh)][n + 1 : P : SLOTS, :], in_=table[(n, iwh)][0:P:SLOTS, :])
+        def multiply_b(n, iwh):
+            multiply_rows(tb[n][:, iwh, :], n, iwh, 1, SIDE, -1)
 
-        def place_squares(n, iwh):
-            rows = T_ROWS - 1
-            source = squares[iwh][n:P:SLOTS, :]
-            nc.sync.dma_start(out=ta[(n, iwh)][0:P:SLOTS, 0 : ROW * rows], in_=source[:, 0 : ROW * rows])
-            nc.sync.dma_start(out=tb[(n, iwh)][0:P:SLOTS, ROW : ROW * (rows + 1)], in_=source[:, 2 * ROW : ROW * (rows + 2)])
+        def spread(n, which, first):
+            rows = slice(ROW * first, ROW * (first + T_ROWS))
+            nc.sync.dma_start(out=which[SPREAD][n + 1 : P : SLOTS, :, rows], in_=which[n][0:P:SLOTS, :, rows])
 
-        def exchange(n, iwh):
-            a, b = ta[(n, iwh)], tb[(n, iwh)]
-            nc.sync.dma_start(out=a[3:P:SLOTS, ROW : ROW + IMAGE_COLS], in_=b[3:P:SLOTS, 0:IMAGE_COLS])
-            nc.sync.dma_start(out=b[1:P:SLOTS, ROW : ROW + IMAGE_COLS], in_=a[1:P:SLOTS, 2 * ROW : 2 * ROW + IMAGE_COLS])
+        def place_squares(n, which):
+            nc.sync.dma_start(out=which[n][0:P:SLOTS], in_=squares[n:P:SLOTS])
+
+        def exchange(n, target, source, slot, first):
+            rows = slice(ROW * first, ROW * (first + GRID))
+            nc.sync.dma_start(out=target[n][slot:P:SLOTS, :, rows], in_=source[n][slot:P:SLOTS, :, rows])
 
         sums = {}
+        results = {}
         done = {}
 
         def warm_tensor(n, table):
@@ -245,11 +192,10 @@ def tile_fast2order_de_conv_kernel(tc, x, W_words, W_scales, out):
         def contract(n, ih, iwh, halves):
             a = 2 * ih + iwh
             width = len(halves) * N_TILE
-            table = (ta if ih < 2 else tb)[(n, iwh)]
-            row = (0, 1, 1, 2)[ih]
+            table = (ta if ih < 2 else tb)[n][:, iwh, :]
             codes = packed.tile([P, HALVES * N_TILE], U32, name="codes", align_bytes=64)
             scales = packed.tile([P, HALVES * N_TILE], U8, name="scales", align_bytes=64)
-            begin = ROW * row + PACK * N_TILE * halves[0]
+            begin = ROW * ih + PACK * N_TILE * halves[0]
             nc.vector.quantize_mx(
                 out=codes[:, 0:width].bitcast(FP8X4), scales=scales[:, 0:width], in_=table[:, begin : begin + PACK * width]
             )
@@ -269,106 +215,135 @@ def tile_fast2order_de_conv_kernel(tc, x, W_words, W_scales, out):
                     )
                     done[(n, half, m)] += 1
 
-        def empty(n, half, emptiers, stores):
+        def empty(n, half):
+            results[(n, half)] = outs.tile([P, M_TILES, TILE_ROWS, QUADS, PHASES], F32, name="result")
             for m in range(M_TILES):
-                result = results.tile([P, TILE_ROWS, QUADS, PHASES], F32, name="result")
-                emptiers[m % len(emptiers)](
-                    out=result[:],
-                    in_=sums[(n, half, m)][:].rearrange("o (y s q) -> o y q s", s=PHASES, y=TILE_ROWS),
-                )
-                stores[m % len(stores)].dma_start(
-                    out=out[n, P * m : P * (m + 1), TILE_ROWS * half : TILE_ROWS * (half + 1), :].rearrange(
+                nc.scalar.copy(out=results[(n, half)][:, m], in_=bank_rows(n, half, m))
+
+        def bank_rows(n, half, m):
+            return sums[(n, half, m)][:].rearrange("o (y s q) -> o y q s", s=PHASES, y=TILE_ROWS)
+
+        def store(n, half):
+            rows = out[n, :, TILE_ROWS * half : TILE_ROWS * (half + 1), :].rearrange("(m o) y z -> o m (y z)", m=M_TILES)
+            nc.sync.dma_start(out=rows, in_=results[(n, half)][:].rearrange("o m y q s -> o m (y q s)"))
+
+        def finish(half, copies):
+            result = outs.tile([P, M_TILES, TILE_ROWS, QUADS, PHASES], F32, name="result")
+            for m in range(M_TILES):
+                copies[m](out=result[:, m], in_=bank_rows(SPREAD, half, m))
+                nc.sync.dma_start(
+                    out=out[SPREAD, P * m : P * (m + 1), TILE_ROWS * half : TILE_ROWS * (half + 1), :].rearrange(
                         "o y z -> o (y z)"
                     ),
-                    in_=result[:].rearrange("o y q s -> o (y q s)"),
+                    in_=result[:, m].rearrange("o y q s -> o (y q s)"),
                 )
 
         both = list(range(HALVES))
 
-        def build_on_scalar(g, b, second):
-            early, windows, late = table_pieces(g, b, second)
-            for destination, source in early + windows + late:
-                nc.scalar.copy(out=destination, in_=source)
-
-        def outer_passes(n, iwh):
-            contract(n, 0, iwh, both)
-            contract(n, 3, iwh, both)
-            exchange(n, iwh)
+        def pass_of(n, ih):
+            for iwh in range(2):
+                contract(n, ih, iwh, both)
 
         def inner_passes(n):
-            for iwh in range(2):
-                contract(n, 1, iwh, both)
-                contract(n, 2, iwh, both)
+            pass_of(n, 1)
+            pass_of(n, 2)
             for half in both:
-                empty(n, half, [nc.scalar.copy], [nc.sync])
+                empty(n, half)
 
-        early, windows, late = table_pieces(0, 0, True)
-        for destination, source in windows[:PHASES]:
-            nc.vector.tensor_copy(out=destination, in_=source)
+        image_rows = x_rows[:].rearrange("p (r w) -> p r w", w=SIDE)
+        for phase in range(PHASES):
+            columns = slice(GRID * phase, GRID * (phase + 1))
+            nc.vector.tensor_copy(out=wins[SQUARES][:, :, columns], in_=image_rows[:, :, phase : phase + GRID])
+        fill_windows(0)
         for iwh in range(2):
-            for k, bank in enumerate(banks):
-                first, last = BANK_ROWS * k, min(SIDE, BANK_ROWS * (k + 1))
-                rows = bank[:, 0 : (last - first) * SIDE].rearrange("p (h w) -> p h w", w=SIDE)
-                for phase in range(PHASES):
+            if iwh == 1:
+                nc.scalar.copy(out=held[SQUARES][:, 1, :, 0:2], in_=held[SQUARES][:, 0, :, 2:PHASES])
+            for k, (first, last) in enumerate(BANKS):
+                rows = banks[k][:, 0 : (last - first) * SIDE].rearrange("p (h w) -> p h w", w=SIDE)
+                for phase in range(2 * iwh, PHASES):
                     shift = 2 * iwh + phase
                     every_fourth = rows[:, :, shift : shift + PACK * (QUADS - 1) + 1 : PACK]
                     nc.scalar.copy(
-                        out=held[0][:, iwh, first:last, phase, :, :],
+                        out=held[SQUARES][:, iwh, first:last, phase],
                         in_=every_fourth.unsqueeze(3).to_broadcast([P, last - first, QUADS, PAIR]),
                     )
-        open_pair(0, 0)
-        multiply_rows(ta[(0, 0)], 0, 0, 0, BANK_ROWS, 0, TOP_ROWS)
-        for destination, source in windows[PHASES:]:
-            nc.vector.tensor_copy(out=destination, in_=source)
-        multiply_rows(tb[(0, 0)], 0, 0, 0, BANK_ROWS - 1, 1, 0)
-        multiply_rows(ta[(0, 0)], 0, 0, BANK_ROWS, T_ROWS, 0, TOP_ROWS)
-        multiply_rows(tb[(0, 0)], 0, 0, BANK_ROWS - 1, T_ROWS, 1, 0)
-        multiply_pair(0, 0, 1)
+                multiply_rows(squares[:, iwh, :], SQUARES, iwh, first, last, 0)
+            fill_held(0, slice(iwh, iwh + 1))
+        for a in (0, 1):
+            load_words(w_words, a)
+        for a in (6, 7, 2, 3, 4, 5):
+            load_words(w_natural, a)
+        fill_windows(1)
+        fill_held(1, slice(0, 2))
+        turn_words(3)
 
-        spread(0, 0)
-        load_pair(1, 0)
-        spread(0, 1)
-        build_on_scalar(1, 1, False)
+        open_pair(0)
         for iwh in range(2):
-            multiply_rows(squares[iwh], 1, iwh, 0, SIDE, 0, 0)
-            place_squares(0, iwh)
-        warm_tensor(0, squares[0])
-        build_on_scalar(2, 0, True)
-        load_pair(2, 1)
-        outer_passes(0, 0)
-        outer_passes(0, 1)
-        load_words(1)
-        load_words(2)
-        for iwh in range(2):
-            place_squares(SPREAD, iwh)
-        build_on_scalar(3, 1, True)
+            multiply_a(0, iwh)
+            multiply_b(0, iwh)
+        spread(0, ta, 0)
+        spread(0, tb, 1)
+        place_squares(0, ta)
+        place_squares(0, tb)
+        turn_words(1)
+        turn_words(2)
 
-        def streams(n, iwh, warm_up=False):
-            multiply_pair(n, n + 1, iwh)
-            if warm_up:
-                warm_tensor(n, tb[(n, iwh)])
-            spread(n, iwh)
-            place_squares(n, iwh)
+        def streams_a(n):
+            open_pair(n)
+            for iwh in range(2):
+                multiply_a(n, iwh)
+            spread(n, ta, 0)
 
-        streams(1, 0, True)
-        streams(1, 1)
+        def streams_b(n):
+            for iwh in range(2):
+                multiply_b(n, iwh)
+            spread(n, tb, 1)
+
+        def outer_passes(n):
+            pass_of(n, 0)
+            exchange(n, ta, tb, 3, 1)
+            pass_of(n, 3)
+            exchange(n, tb, ta, 1, 2)
+
+        streams_a(1)
+        warm_tensor(0, ta[1][:, 0, :])
+        outer_passes(0)
+        fill_windows(2)
+        fill_held(2, slice(0, 2))
+        streams_b(1)
+        warm_tensor(1, tb[1][:, 0, ROW:])
+        place_squares(1, ta)
+        place_squares(1, tb)
+        for which in (ta, tb):
+            place_squares(SPREAD, which)
         inner_passes(0)
-        streams(2, 0)
-        outer_passes(1, 0)
-        outer_passes(1, 1)
-        streams(2, 1)
+        streams_a(2)
+        outer_passes(1)
+        place_squares(2, ta)
+        for half in both:
+            store(0, half)
+        streams_b(2)
+        warm_tensor(2, tb[2][:, 0, ROW:])
+        place_squares(2, tb)
         inner_passes(1)
-        outer_passes(2, 0)
-        outer_passes(2, 1)
-
-        outer_passes(SPREAD, 0)
-        outer_passes(SPREAD, 1)
+        pass_of(2, 0)
+        exchange(2, ta, tb, 3, 1)
+        pass_of(SPREAD, 0)
+        exchange(SPREAD, ta, tb, 3, 1)
+        pass_of(2, 3)
+        exchange(2, tb, ta, 1, 2)
+        for half in both:
+            store(1, half)
+        pass_of(SPREAD, 3)
+        exchange(SPREAD, tb, ta, 1, 2)
         inner_passes(2)
-        contract(SPREAD, 1, 0, both)
+        for half in both:
+            store(2, half)
+
+        for iwh in range(2):
+            contract(SPREAD, 1, iwh, both)
         contract(SPREAD, 2, 0, both)
-        contract(SPREAD, 1, 1, [0])
         contract(SPREAD, 2, 1, [0])
-        empty(SPREAD, 0, [nc.scalar.copy], [nc.sync])
-        contract(SPREAD, 1, 1, [1])
+        finish(0, [nc.scalar.copy, nc.scalar.copy])
         contract(SPREAD, 2, 1, [1])
-        empty(SPREAD, 1, [nc.scalar.copy, nc.vector.tensor_copy], [nc.sync])
+        finish(1, [nc.scalar.copy, nc.vector.tensor_copy])

@@ -34,6 +34,12 @@ ROW = GRID * PACK
 IMAGE_COLS = GRID * ROW
 T_ROWS = GRID + 2
 TABLE = SIDE * ROW
+LOWER = GRID * PAIR
+GROUP = 2 * QUADS
+EDGE_ROW = 2 * PAIR
+HELD = SIDE * LOWER
+SECOND, FIRST, EDGES = 0, TABLE + ROW, 2 * TABLE + ROW
+STORE = EDGES + SIDE * EDGE_ROW
 TOP_ROWS = 3
 WIN_ROWS = TOP_ROWS + T_ROWS
 BANKS = [(0, 7), (7, 21), (21, 35)]
@@ -60,6 +66,11 @@ def tile_fast2order_de_conv_kernel(tc, x, W_words, W_scales, out):
         warm = keep.tile([P, 2, 8], BF16)
         nc.gpsimd.memset(warm[:, 0, :], 0.0)
         nc.scalar.copy(out=warm[:, 1, :], in_=warm[:, 0, :])
+        zeros = keep.tile([P, N_TILE], BF16)
+        nc.gpsimd.memset(zeros[:].bitcast(U32), 0)
+        idle = psum.tile([P, N_TILE], F32, name="sums11")
+        for repeat in range(4):
+            nc.tensor.matmul(out=idle[:], lhsT=zeros[:, 0:P], rhs=zeros[:], start=True, stop=True)
         w_planes = keep.tile([P, PASSES, OUT_CH], U8, align_bytes=64)
         nc.vector.memset(w_planes[:].bitcast(I32), 0)
 
@@ -96,32 +107,33 @@ def tile_fast2order_de_conv_kernel(tc, x, W_words, W_scales, out):
                 out=w_planes[32 * quadrant : 32 * quadrant + 4].rearrange("p a o -> p (a o)").bitcast(I32),
                 in_=scale_rows[4 * quadrant : 4 * quadrant + 4, :].bitcast(I32),
             )
-        w_words = keep.tile([P, PASSES, 2 * OUT_CH], U8, align_bytes=64)
+        w_words = [keep.tile([P, 2, 2 * OUT_CH], U8, name="w_words%d" % ih, align_bytes=64) for ih in range(SLOTS)]
         words_by_pass = W_words.rearrange("g (c2 a r) b -> a (g c2) r b", c2=2, a=PASSES)
         w_natural = keep.tile([P, PASSES, 2 * OUT_CH], U8, align_bytes=64)
 
         def load_words(target, a):
-            nc.sync.dma_start(out=target[:, a, :].bitcast(I32), in_=words_by_pass[a].bitcast(I32))
+            nc.sync.dma_start(out=target.bitcast(I32), in_=words_by_pass[a].bitcast(I32))
 
         def turn_words(ih):
             for slot in range(SLOTS):
                 jh = (slot + ih) % SLOTS
                 two = slice(2 * ih, 2 * ih + 2)
                 nc.sync.dma_start(
-                    out=w_words[slot:P:SLOTS, two, :].rearrange("p a o -> p (a o)").bitcast(I32),
+                    out=w_words[ih][slot:P:SLOTS].rearrange("p a o -> p (a o)").bitcast(I32),
                     in_=w_natural[jh:P:SLOTS, two, :].rearrange("p a o -> p (a o)").bitcast(I32),
                 )
 
-        for a in (0, 1):
-            load_words(w_words, a)
-        for a in (6, 7, 2, 3, 4, 5):
-            load_words(w_natural, a)
-
-        held = {}
         wins = {}
-        held[SQUARES] = keep.tile([P, 2, SIDE, PHASES, QUADS, PAIR], BF16, name="held_squares")
+        held_tiles = [keep.tile([P, HELD + SIDE * EDGE_ROW], BF16, name="held%d" % b) for b in range(3)]
+        second_squares = keep.tile([P, SIDE, LOWER], BF16)
+
+        def held_tile(n):
+            return held_tiles[2 if n == SQUARES else n % 2]
+
+        def held_rows(n, iwh):
+            return second_squares[:] if iwh else held_tile(n)[:, 0:HELD].rearrange("p (u e) -> p u e", e=LOWER)
+
         wins[SQUARES] = keep.tile([P, SIDE, ROW], BF16, name="wins_squares")
-        spare_held = [keep.tile([P, 2, SIDE, PHASES, QUADS, PAIR], BF16, name="held%d" % b) for b in range(2)]
         spare_wins = [keep.tile([P, WIN_ROWS, ROW], BF16, name="wins%d" % b) for b in range(2)]
         for b in range(2):
             nc.gpsimd.memset(spare_wins[b][:, 0:2, :], 0.0)
@@ -136,14 +148,13 @@ def tile_fast2order_de_conv_kernel(tc, x, W_words, W_scales, out):
                     out=wins[n][slot:P:SLOTS, place : place + SIDE, :], in_=wins[SQUARES][image:P:SLOTS, :, :]
                 )
 
-        def fill_held(n, pairs):
-            held[n] = spare_held[n % 2]
+        def fill_held(n):
             for slot in range(SLOTS):
                 image = n if slot else SPREAD
-                nc.sync.dma_start(out=held[n][slot:P:SLOTS, pairs], in_=held[SQUARES][image:P:SLOTS, pairs])
+                nc.sync.dma_start(out=held_tile(n)[slot:P:SLOTS], in_=held_tile(SQUARES)[image:P:SLOTS])
 
         def multiply_rows(table, g, iwh, first, last, below):
-            pairs = held[g][:, iwh, first:last, :, :, :].rearrange("p u f q t -> p (u f q) t")
+            pairs = held_rows(g, iwh)[:, first:last, :].rearrange("p u (w t) -> p (u w) t", t=PAIR)
             words = wins[g][:, first + below : last + below, :].rearrange("p u e -> p (u e)")
             nc.vector.tensor_tensor(
                 out=table[:, ROW * first : ROW * last].rearrange("p (w r t) -> p w r t", r=PACK // PAIR, t=PAIR),
@@ -152,30 +163,97 @@ def tile_fast2order_de_conv_kernel(tc, x, W_words, W_scales, out):
                 op=mybir.AluOpType.mult,
             )
 
-        ta = {SPREAD: keep.tile([P, 2, TABLE], BF16, name="ta_spread", align_bytes=64)}
-        tb = {SPREAD: keep.tile([P, 2, TABLE], BF16, name="tb_spread", align_bytes=64)}
-        squares = keep.tile([P, 2, TABLE], BF16, align_bytes=64)
+        ta = {}
+        tb = {}
+        squares = {}
+        for iwh in range(2):
+            ta[(SPREAD, iwh)] = keep.tile([P, TABLE], BF16, name="ta_spread%d" % iwh, align_bytes=64)
+            tb[(SPREAD, iwh)] = keep.tile([P, TABLE], BF16, name="tb_spread%d" % iwh, align_bytes=64)
+            squares[iwh] = keep.tile([P, TABLE], BF16, name="squares%d" % iwh, align_bytes=64)
 
-        def open_pair(n):
-            ta[n] = prods.tile([P, 2, TABLE], BF16, name="ta", align_bytes=64)
-            tb[n] = prods.tile([P, 2, TABLE], BF16, name="tb", align_bytes=64)
+        stores = {}
 
-        def multiply_a(n, iwh):
-            multiply_rows(ta[n][:, iwh, :], n, iwh, 0, T_ROWS, TOP_ROWS)
+        def open_store(n, which):
+            name = "ta" if which is ta else "tb"
+            stores[(n, name)] = prods.tile([P, STORE], BF16, name=name, align_bytes=64)
+            for iwh, begin in enumerate((FIRST, SECOND)):
+                which[(n, iwh)] = stores[(n, name)][:, begin : begin + TABLE]
 
-        def multiply_b(n, iwh):
-            multiply_rows(tb[n][:, iwh, :], n, iwh, 1, SIDE, -1)
+        def span(which):
+            return (0, T_ROWS, TOP_ROWS) if which is ta else (1, SIDE, 0)
 
-        def spread(n, which, first):
+        def multiply_words(n, which, iwh):
+            first, last, window_row = span(which)
+            multiply_rows(which[(n, iwh)], n, iwh, first, last, window_row - first)
+
+        second_held = keep.tile([P, SIDE, LOWER], BF16)
+        lower_wins = keep.tile([P, WIN_ROWS, LOWER], BF16)
+
+        def derive(n):
+            first_words = held_rows(n, 0).bitcast(F32)
+            second_words = second_held[:].bitcast(F32)
+            nc.scalar.copy(
+                out=second_words[:, :, 0 : GRID - 2].rearrange("p u (w g) -> p u w g", g=2),
+                in_=first_words[:, :, 1 : GRID - 1].rearrange("p u (g w) -> p u w g", g=2),
+            )
+            nc.scalar.copy(out=second_words[:, :, GRID - 1 : GRID], in_=first_words[:, :, GRID - 1 : GRID])
+            beyond = held_tile(n)[:, HELD:].bitcast(F32).rearrange("p (u f) -> p u f", f=2)
+            nc.scalar.copy(out=second_words[:, :, GROUP - 2 : GRID : GROUP], in_=beyond)
+            lower = wins[n][:].bitcast(F32)[:, :, 0 : ROW // 2 : 2]
+            nc.scalar.copy(
+                out=lower_wins[:].bitcast(F32).rearrange("p u (w g) -> p u w g", g=2),
+                in_=lower.rearrange("p u (g w) -> p u w g", g=2)[:, :, :, ::-1],
+            )
+
+        def multiply_lower(n, which):
+            first, last, begin = span(which)
+            end = begin + last - first
+            nc.vector.tensor_tensor(
+                out=which[(n, 1)].rearrange("p (u e) -> p u e", e=ROW)[:, first:last, LOWER:ROW],
+                in0=second_held[:, first:last, :],
+                in1=lower_wins[:, begin:end, :],
+                op=mybir.AluOpType.mult,
+            )
+            words = wins[n][:, begin:end, :].rearrange("p u (f q r t) -> p u f q r t", f=PHASES, q=QUADS, r=2)
+            edges = stores[(n, "ta" if which is ta else "tb")][:, EDGES:STORE]
+            nc.vector.tensor_tensor(
+                out=edges.rearrange("p (u f t) -> p u f t", f=2, t=PAIR)[:, first:last],
+                in0=second_held[:, first:last, :].rearrange("p u (f q g t) -> p u f q g t", f=2, q=QUADS, g=2)[
+                    :, :, :, QUADS - 1, 0, :
+                ],
+                in1=words[:, :, 2:PHASES, QUADS - 1, 1, :],
+                op=mybir.AluOpType.mult,
+            )
+
+        def compose(n, which):
+            first, last, begin = span(which)
+            row = ROW // 2
+            words = stores[(n, "ta" if which is ta else "tb")][:].bitcast(F32)
+            out_rows = words[:, 0 : TABLE // 2].rearrange("p (u e) -> p u e", e=row)[:, first:last]
+            for group in range(2):
+                lower = row * first + row // 2 + (1 - group)
+                step = FIRST // 2 + row * first + (GRID if group == 0 else PAIR) - lower
+                two = words[:, 0 : 2 * step].rearrange("p (r s) -> p r s", r=2)
+                source = two[:, :, lower : lower + row * (last - first)].rearrange("p r (u e) -> p u e r", e=row)
+                nc.scalar.copy(
+                    out=out_rows[:, :, GRID * group : GRID * (group + 1)].rearrange("p u (w r) -> p u w r", r=2),
+                    in_=source[:, :, 0:GRID:2, :],
+                )
+            edges = words[:, EDGES // 2 : STORE // 2].rearrange("p (u f) -> p u f", f=2)
+            nc.scalar.copy(out=out_rows[:, :, 3 * GRID // 2 - 1 :: GRID // 2], in_=edges[:, first:last])
+
+        def spread(n, which, iwh):
+            first = 0 if which is ta else 1
             rows = slice(ROW * first, ROW * (first + T_ROWS))
-            nc.sync.dma_start(out=which[SPREAD][n + 1 : P : SLOTS, :, rows], in_=which[n][0:P:SLOTS, :, rows])
+            nc.sync.dma_start(out=which[(SPREAD, iwh)][n + 1 : P : SLOTS, rows], in_=which[(n, iwh)][0:P:SLOTS, rows])
 
-        def place_squares(n, which):
-            nc.sync.dma_start(out=which[n][0:P:SLOTS], in_=squares[n:P:SLOTS])
+        def place_squares(n, which, iwh):
+            nc.sync.dma_start(out=which[(n, iwh)][0:P:SLOTS], in_=squares[iwh][n:P:SLOTS])
 
-        def exchange(n, target, source, slot, first):
-            rows = slice(ROW * first, ROW * (first + GRID))
-            nc.sync.dma_start(out=target[n][slot:P:SLOTS, :, rows], in_=source[n][slot:P:SLOTS, :, rows])
+        def exchange(n, ih, iwh):
+            target, source, slot = (ta, tb, 3) if ih == 1 else (tb, ta, 1)
+            rows = slice(ROW * ih, ROW * (ih + GRID))
+            nc.sync.dma_start(out=target[(n, iwh)][slot:P:SLOTS, rows], in_=source[(n, iwh)][slot:P:SLOTS, rows])
 
         sums = {}
         results = {}
@@ -192,7 +270,7 @@ def tile_fast2order_de_conv_kernel(tc, x, W_words, W_scales, out):
         def contract(n, ih, iwh, halves):
             a = 2 * ih + iwh
             width = len(halves) * N_TILE
-            table = (ta if ih < 2 else tb)[n][:, iwh, :]
+            table = (ta if ih < 2 else tb)[(n, iwh)]
             codes = packed.tile([P, HALVES * N_TILE], U32, name="codes", align_bytes=64)
             scales = packed.tile([P, HALVES * N_TILE], U8, name="scales", align_bytes=64)
             begin = ROW * ih + PACK * N_TILE * halves[0]
@@ -206,7 +284,7 @@ def tile_fast2order_de_conv_kernel(tc, x, W_words, W_scales, out):
                         done[(n, half, m)] = 0
                     nc.tensor.matmul_mx(
                         out=sums[(n, half, m)][:],
-                        lhsT=w_words[:, a, 2 * P * m : 2 * P * (m + 1)].bitcast(FP4X4),
+                        lhsT=w_words[ih][:, iwh, 2 * P * m : 2 * P * (m + 1)].bitcast(FP4X4),
                         lhsT_scale=w_planes[:, a, P * m : P * (m + 1)],
                         rhs=codes[:, N_TILE * place : N_TILE * (place + 1)].bitcast(FP8X4),
                         rhs_scale=scales[:, N_TILE * place : N_TILE * (place + 1)],
@@ -231,6 +309,7 @@ def tile_fast2order_de_conv_kernel(tc, x, W_words, W_scales, out):
             result = outs.tile([P, M_TILES, TILE_ROWS, QUADS, PHASES], F32, name="result")
             for m in range(M_TILES):
                 copies[m](out=result[:, m], in_=bank_rows(SPREAD, half, m))
+            for m in range(M_TILES):
                 nc.sync.dma_start(
                     out=out[SPREAD, P * m : P * (m + 1), TILE_ROWS * half : TILE_ROWS * (half + 1), :].rearrange(
                         "o y z -> o (y z)"
@@ -255,87 +334,118 @@ def tile_fast2order_de_conv_kernel(tc, x, W_words, W_scales, out):
             columns = slice(GRID * phase, GRID * (phase + 1))
             nc.vector.tensor_copy(out=wins[SQUARES][:, :, columns], in_=image_rows[:, :, phase : phase + GRID])
         fill_windows(0)
-        for iwh in range(2):
-            if iwh == 1:
-                nc.scalar.copy(out=held[SQUARES][:, 1, :, 0:2], in_=held[SQUARES][:, 0, :, 2:PHASES])
-            for k, (first, last) in enumerate(BANKS):
-                rows = banks[k][:, 0 : (last - first) * SIDE].rearrange("p (h w) -> p h w", w=SIDE)
-                for phase in range(2 * iwh, PHASES):
-                    shift = 2 * iwh + phase
-                    every_fourth = rows[:, :, shift : shift + PACK * (QUADS - 1) + 1 : PACK]
-                    nc.scalar.copy(
-                        out=held[SQUARES][:, iwh, first:last, phase],
-                        in_=every_fourth.unsqueeze(3).to_broadcast([P, last - first, QUADS, PAIR]),
-                    )
-                multiply_rows(squares[:, iwh, :], SQUARES, iwh, first, last, 0)
-            fill_held(0, slice(iwh, iwh + 1))
-        for a in (0, 1):
-            load_words(w_words, a)
-        for a in (6, 7, 2, 3, 4, 5):
-            load_words(w_natural, a)
+
+        def copy_held(k, iwh, phase):
+            first, last = BANKS[k]
+            rows = banks[k][:, 0 : (last - first) * SIDE].rearrange("p (h w) -> p h w", w=SIDE)
+            shift = 2 * iwh + phase
+            every_fourth = rows[:, :, shift : shift + PACK * (QUADS - 1) + 1 : PACK]
+            target = held_rows(SQUARES, iwh)[:, first:last, :].rearrange("p u (f q t) -> p u f q t", f=PHASES, q=QUADS)
+            nc.scalar.copy(
+                out=target[:, :, phase], in_=every_fourth.unsqueeze(3).to_broadcast([P, last - first, QUADS, PAIR])
+            )
+
+        for k, (first, last) in enumerate(BANKS):
+            for phase in range(PHASES):
+                copy_held(k, 0, phase)
+            multiply_rows(squares[0], SQUARES, 0, first, last, 0)
+        beyond = held_tile(SQUARES)[:, HELD:].rearrange("p (u f t) -> p u f t", f=2, t=PAIR)
+        for k, (first, last) in enumerate(BANKS):
+            rows = banks[k][:, 0 : (last - first) * SIDE].rearrange("p (h w) -> p h w", w=SIDE)
+            nc.scalar.copy(
+                out=beyond[:, first:last],
+                in_=rows[:, :, GRID : GRID + 2].unsqueeze(3).to_broadcast([P, last - first, 2, PAIR]),
+            )
+        fill_held(0)
+        nc.vector.tensor_copy(
+            out=held_rows(SQUARES, 1)[:, :, 0 : LOWER // 2], in_=held_rows(SQUARES, 0)[:, :, LOWER // 2 :]
+        )
+        for k, (first, last) in enumerate(BANKS):
+            for phase in range(2, PHASES):
+                copy_held(k, 1, phase)
+            multiply_rows(squares[1], SQUARES, 1, first, last, 0)
+        derive(0)
         fill_windows(1)
-        fill_held(1, slice(0, 2))
-        turn_words(3)
+        fill_held(1)
+        for a in (0, 1):
+            load_words(w_words[0][:, a, :], a)
+        for a in (6, 7, 2, 3, 4, 5):
+            load_words(w_natural[:, a, :], a)
 
-        open_pair(0)
-        for iwh in range(2):
-            multiply_a(0, iwh)
-            multiply_b(0, iwh)
-        spread(0, ta, 0)
-        spread(0, tb, 1)
-        place_squares(0, ta)
-        place_squares(0, tb)
-        turn_words(1)
-        turn_words(2)
+        def streams(n, which):
+            open_store(n, which)
+            multiply_words(n, which, 0)
+            multiply_lower(n, which)
+            compose(n, which)
 
-        def streams_a(n):
-            open_pair(n)
+        def spread_both(n, which):
             for iwh in range(2):
-                multiply_a(n, iwh)
-            spread(n, ta, 0)
+                spread(n, which, iwh)
 
-        def streams_b(n):
+        def place_both(n, which):
             for iwh in range(2):
-                multiply_b(n, iwh)
-            spread(n, tb, 1)
+                place_squares(n, which, iwh)
 
-        def outer_passes(n):
-            pass_of(n, 0)
-            exchange(n, ta, tb, 3, 1)
-            pass_of(n, 3)
-            exchange(n, tb, ta, 1, 2)
+        def exchange_both(n, ih):
+            for iwh in range(2):
+                exchange(n, ih, iwh)
 
-        streams_a(1)
-        warm_tensor(0, ta[1][:, 0, :])
-        outer_passes(0)
-        fill_windows(2)
-        fill_held(2, slice(0, 2))
-        streams_b(1)
-        warm_tensor(1, tb[1][:, 0, ROW:])
-        place_squares(1, ta)
-        place_squares(1, tb)
+        streams(0, ta)
+        for ih in (3, 1, 2):
+            turn_words(ih)
+        streams(0, tb)
+        derive(1)
+        spread_both(0, ta)
+        place_both(0, ta)
+        spread_both(0, tb)
+        place_both(0, tb)
         for which in (ta, tb):
-            place_squares(SPREAD, which)
+            open_store(1, which)
+            multiply_words(1, which, 0)
+        warm_tensor(0, tb[(1, 0)][:, ROW:])
+        pass_of(0, 0)
+        exchange_both(0, 1)
+        fill_windows(2)
+        multiply_lower(1, ta)
+        compose(1, ta)
+        pass_of(0, 3)
+        exchange_both(0, 2)
+        fill_held(2)
+        spread_both(1, ta)
+        multiply_lower(1, tb)
+        compose(1, tb)
+        place_both(1, ta)
+        derive(2)
+        spread_both(1, tb)
         inner_passes(0)
-        streams_a(2)
-        outer_passes(1)
-        place_squares(2, ta)
+        place_both(1, tb)
+        for which in (ta, tb):
+            place_both(SPREAD, which)
+        streams(2, ta)
+        warm_tensor(1, ta[(2, 0)])
         for half in both:
             store(0, half)
-        streams_b(2)
-        warm_tensor(2, tb[2][:, 0, ROW:])
-        place_squares(2, tb)
+        pass_of(1, 0)
+        exchange_both(1, 1)
+        spread_both(2, ta)
+        pass_of(1, 3)
+        exchange_both(1, 2)
+        place_both(2, ta)
+        streams(2, tb)
+        warm_tensor(2, tb[(2, 0)][:, ROW:])
         inner_passes(1)
+        spread_both(2, tb)
+        place_both(2, tb)
         pass_of(2, 0)
-        exchange(2, ta, tb, 3, 1)
+        exchange_both(2, 1)
         pass_of(SPREAD, 0)
-        exchange(SPREAD, ta, tb, 3, 1)
+        exchange_both(SPREAD, 1)
         pass_of(2, 3)
-        exchange(2, tb, ta, 1, 2)
+        exchange_both(2, 2)
         for half in both:
             store(1, half)
         pass_of(SPREAD, 3)
-        exchange(SPREAD, tb, ta, 1, 2)
+        exchange_both(SPREAD, 2)
         inner_passes(2)
         for half in both:
             store(2, half)

@@ -123,6 +123,11 @@ def tile_fast2order_de_conv_kernel(tc, x, W_words, W_scales, out):
                     in_=w_natural[jh:P:SLOTS, two, :].rearrange("p a o -> p (a o)").bitcast(I32),
                 )
 
+        for a in (0, 1):
+            load_words(w_words[0][:, a, :], a)
+        for a in (6, 7, 2, 3, 4, 5):
+            load_words(w_natural[:, a, :], a)
+
         wins = {}
         held_tiles = [keep.tile([P, HELD + SIDE * EDGE_ROW], BF16, name="held%d" % b) for b in range(3)]
         second_squares = keep.tile([P, SIDE, LOWER], BF16)
@@ -190,6 +195,11 @@ def tile_fast2order_de_conv_kernel(tc, x, W_words, W_scales, out):
         lower_wins = keep.tile([P, WIN_ROWS, LOWER], BF16)
 
         def derive(n):
+            lower = wins[n][:].bitcast(F32)[:, :, 0 : ROW // 2 : 2]
+            nc.scalar.copy(
+                out=lower_wins[:].bitcast(F32).rearrange("p u (w g) -> p u w g", g=2),
+                in_=lower.rearrange("p u (g w) -> p u w g", g=2)[:, :, :, ::-1],
+            )
             first_words = held_rows(n, 0).bitcast(F32)
             second_words = second_held[:].bitcast(F32)
             nc.scalar.copy(
@@ -199,11 +209,6 @@ def tile_fast2order_de_conv_kernel(tc, x, W_words, W_scales, out):
             nc.scalar.copy(out=second_words[:, :, GRID - 1 : GRID], in_=first_words[:, :, GRID - 1 : GRID])
             beyond = held_tile(n)[:, HELD:].bitcast(F32).rearrange("p (u f) -> p u f", f=2)
             nc.scalar.copy(out=second_words[:, :, GROUP - 2 : GRID : GROUP], in_=beyond)
-            lower = wins[n][:].bitcast(F32)[:, :, 0 : ROW // 2 : 2]
-            nc.scalar.copy(
-                out=lower_wins[:].bitcast(F32).rearrange("p u (w g) -> p u w g", g=2),
-                in_=lower.rearrange("p u (g w) -> p u w g", g=2)[:, :, :, ::-1],
-            )
 
         def multiply_lower(n, which):
             first, last, begin = span(which)
@@ -334,6 +339,7 @@ def tile_fast2order_de_conv_kernel(tc, x, W_words, W_scales, out):
             columns = slice(GRID * phase, GRID * (phase + 1))
             nc.vector.tensor_copy(out=wins[SQUARES][:, :, columns], in_=image_rows[:, :, phase : phase + GRID])
         fill_windows(0)
+        turn_words(3)
 
         def copy_held(k, iwh, phase):
             first, last = BANKS[k]
@@ -367,10 +373,8 @@ def tile_fast2order_de_conv_kernel(tc, x, W_words, W_scales, out):
         derive(0)
         fill_windows(1)
         fill_held(1)
-        for a in (0, 1):
-            load_words(w_words[0][:, a, :], a)
-        for a in (6, 7, 2, 3, 4, 5):
-            load_words(w_natural[:, a, :], a)
+        for ih in (1, 2):
+            turn_words(ih)
 
         def streams(n, which):
             open_store(n, which)
@@ -391,11 +395,10 @@ def tile_fast2order_de_conv_kernel(tc, x, W_words, W_scales, out):
                 exchange(n, ih, iwh)
 
         streams(0, ta)
-        for ih in (3, 1, 2):
-            turn_words(ih)
         streams(0, tb)
         derive(1)
         spread_both(0, ta)
+        fill_held(2)
         place_both(0, ta)
         spread_both(0, tb)
         place_both(0, tb)
@@ -410,13 +413,12 @@ def tile_fast2order_de_conv_kernel(tc, x, W_words, W_scales, out):
         compose(1, ta)
         pass_of(0, 3)
         exchange_both(0, 2)
-        fill_held(2)
         spread_both(1, ta)
         multiply_lower(1, tb)
         compose(1, tb)
-        place_both(1, ta)
         derive(2)
         spread_both(1, tb)
+        place_both(1, ta)
         inner_passes(0)
         place_both(1, tb)
         for which in (ta, tb):

from contextlib import ExitStack

import concourse.mybir as mybir
from concourse.masks import make_identity

BF16 = mybir.dt.bfloat16
F32 = mybir.dt.float32
I32 = mybir.dt.int32
U8 = mybir.dt.uint8
U32 = mybir.dt.uint32
FP8X4 = mybir.dt.float8_e4m3fn_x4
FP4X4 = mybir.dt.float4_e2m1fn_x4

P = 128
PACK = 4
PAIR = 2
IMAGES = 4
SPREAD = IMAGES - 1
SLOTS = 4
SQUARES = SPREAD + 1
CHANNELS = 16
SIDE = 35
PIXELS = SIDE * SIDE
GRID = 32
QUADS = GRID // PACK
PHASES = PACK
PASSES = 8
TILE_ROWS = 16
N_TILE = TILE_ROWS * GRID
HALVES = GRID // TILE_ROWS
OUT_CH = 256
M_TILES = OUT_CH // P
ROW = GRID * PACK
IMAGE_COLS = GRID * ROW
T_ROWS = GRID + 2
TABLE = SIDE * ROW
LOWER = GRID * PAIR
GROUP = 2 * QUADS
EDGE_ROW = 2 * PAIR
HELD = SIDE * LOWER
SECOND, FIRST, EDGES = 0, TABLE + ROW, 2 * TABLE + ROW
STORE = EDGES + SIDE * EDGE_ROW
TOP_ROWS = 3
WIN_ROWS = TOP_ROWS + T_ROWS
BANKS = [(0, 7), (7, 21), (21, 35)]
WARM_UPS = 6
FLOPS = 2 * IMAGES * GRID * GRID * CHANNELS * 256 * OUT_CH


def tile_fast2order_de_conv_kernel(tc, x, W_words, W_scales, out):
    nc = tc.nc
    with ExitStack() as ctx:
        ctx.enter_context(tc.manual_schedule())
        keep = ctx.enter_context(tc.tile_pool(name="keep", bufs=1))
        prods = ctx.enter_context(tc.tile_pool(name="prods", bufs=2))
        packed = ctx.enter_context(tc.tile_pool(name="packed", bufs=4))
        outs = ctx.enter_context(tc.tile_pool(name="outs", bufs=4))
        psum = ctx.enter_context(tc.psum_pool(name="psum", bufs=2))

        x_flat = x.rearrange("n c h w -> n c (h w)")
        x_rows = keep.tile([P, PIXELS], BF16)
        for slot in range(SLOTS):
            nc.sync.dma_start(
                out=x_rows[slot:P:SLOTS, :], in_=x_flat[slot].unsqueeze(1).to_broadcast([CHANNELS, 2, PIXELS])
            )
        warm = keep.tile([P, 2, 8], BF16)
        nc.gpsimd.memset(warm[:, 0, :], 0.0)
        nc.scalar.copy(out=warm[:, 1, :], in_=warm[:, 0, :])
        zeros = keep.tile([P, N_TILE], BF16)
        nc.gpsimd.memset(zeros[:].bitcast(U32), 0)
        idle = psum.tile([P, N_TILE], F32, name="sums11")
        for repeat in range(4):
            nc.tensor.matmul(out=idle[:], lhsT=zeros[:, 0:P], rhs=zeros[:], start=True, stop=True)
        w_planes = keep.tile([P, PASSES, OUT_CH], U8, align_bytes=64)
        nc.vector.memset(w_planes[:].bitcast(I32), 0)

        identity = keep.tile([P, P], BF16)
        make_identity(nc, identity[:])
        banks = []
        pickers = []
        for iw0 in range(2):
            picker = keep.tile([P, P], BF16, name="picker%d" % iw0)
            nc.vector.memset(picker[:], 0.0)
            by_iw0 = "k (c i s) -> k c i s"
            nc.vector.tensor_copy(
                out=picker[:].rearrange(by_iw0, i=2, s=SLOTS)[:, :, iw0, :],
                in_=identity[:].rearrange(by_iw0, i=2, s=SLOTS)[:, :, iw0, :],
            )
            pickers.append(picker)
        for (first, last), tag in zip(BANKS, ("sums00", "sums01", "sums10")):
            columns = min(SIDE * last, PIXELS - 1) - SIDE * first
            bank = psum.tile([P, N_TILE], F32, name=tag)
            for iw0 in range(2):
                begin = SIDE * first + iw0
                nc.tensor.matmul(
                    out=bank[:, 0:columns],
                    lhsT=pickers[iw0][:],
                    rhs=x_rows[:, begin : begin + columns],
                    start=(iw0 == 0),
                    stop=(iw0 == 1),
                )
            banks.append(bank)

        scale_rows = W_scales.rearrange("g (c2 a) o -> (g c2) (a o)", c2=2)
        for quadrant in range(4):
            nc.sync.dma_start(
                out=w_planes[32 * quadrant : 32 * quadrant + 4].rearrange("p a o -> p (a o)").bitcast(I32),
                in_=scale_rows[4 * quadrant : 4 * quadrant + 4, :].bitcast(I32),
            )
        w_words = [keep.tile([P, 2, 2 * OUT_CH], U8, name="w_words%d" % ih, align_bytes=64) for ih in range(SLOTS)]
        words_by_pass = W_words.rearrange("g (c2 a r) b -> a (g c2) r b", c2=2, a=PASSES)
        w_natural = keep.tile([P, PASSES, 2 * OUT_CH], U8, align_bytes=64)

        def load_words(target, a):
            nc.sync.dma_start(out=target.bitcast(I32), in_=words_by_pass[a].bitcast(I32))

        def turn_words(ih):
            for slot in range(SLOTS):
                jh = (slot + ih) % SLOTS
                two = slice(2 * ih, 2 * ih + 2)
                nc.sync.dma_start(
                    out=w_words[ih][slot:P:SLOTS].rearrange("p a o -> p (a o)").bitcast(I32),
                    in_=w_natural[jh:P:SLOTS, two, :].rearrange("p a o -> p (a o)").bitcast(I32),
                )

        for a in (0, 1):
            load_words(w_words[0][:, a, :], a)
        for a in (6, 7, 2, 3, 4, 5):
            load_words(w_natural[:, a, :], a)

        wins = {}
        held_tiles = [keep.tile([P, HELD + SIDE * EDGE_ROW], BF16, name="held%d" % b) for b in range(3)]
        second_squares = keep.tile([P, SIDE, LOWER], BF16)

        def held_tile(n):
            return held_tiles[2 if n == SQUARES else n % 2]

        def held_rows(n, iwh):
            return second_squares[:] if iwh else held_tile(n)[:, 0:HELD].rearrange("p (u e) -> p u e", e=LOWER)

        wins[SQUARES] = keep.tile([P, SIDE, ROW], BF16, name="wins_squares")
        spare_wins = [keep.tile([P, WIN_ROWS, ROW], BF16, name="wins%d" % b) for b in range(2)]
        for b in range(2):
            nc.gpsimd.memset(spare_wins[b][:, 0:2, :], 0.0)
            nc.gpsimd.memset(spare_wins[b][:, SIDE:WIN_ROWS, :], 0.0)

        def fill_windows(n):
            wins[n] = spare_wins[n % 2]
            for slot in range(SLOTS):
                place = TOP_ROWS - (slot if slot else n + 1)
                image = n if slot else SPREAD
                nc.sync.dma_start(
                    out=wins[n][slot:P:SLOTS, place : place + SIDE, :], in_=wins[SQUARES][image:P:SLOTS, :, :]
                )

        def fill_held(n):
            for slot in range(SLOTS):
                image = n if slot else SPREAD
                nc.sync.dma_start(out=held_tile(n)[slot:P:SLOTS], in_=held_tile(SQUARES)[image:P:SLOTS])

        def multiply_rows(table, g, iwh, first, last, below):
            pairs = held_rows(g, iwh)[:, first:last, :].rearrange("p u (w t) -> p (u w) t", t=PAIR)
            words = wins[g][:, first + below : last + below, :].rearrange("p u e -> p (u e)")
            nc.vector.tensor_tensor(
                out=table[:, ROW * first : ROW * last].rearrange("p (w r t) -> p w r t", r=PACK // PAIR, t=PAIR),
                in0=pairs.unsqueeze(2).to_broadcast([P, (last - first) * GRID, PACK // PAIR, PAIR]),
                in1=words.rearrange("p (w r t) -> p w r t", r=PACK // PAIR, t=PAIR),
                op=mybir.AluOpType.mult,
            )

        ta = {}
        tb = {}
        squares = {}
        for iwh in range(2):
            ta[(SPREAD, iwh)] = keep.tile([P, TABLE], BF16, name="ta_spread%d" % iwh, align_bytes=64)
            tb[(SPREAD, iwh)] = keep.tile([P, TABLE], BF16, name="tb_spread%d" % iwh, align_bytes=64)
            squares[iwh] = keep.tile([P, TABLE], BF16, name="squares%d" % iwh, align_bytes=64)

        stores = {}

        def open_store(n, which):
            name = "ta" if which is ta else "tb"
            stores[(n, name)] = prods.tile([P, STORE], BF16, name=name, align_bytes=64)
            for iwh, begin in enumerate((FIRST, SECOND)):
                which[(n, iwh)] = stores[(n, name)][:, begin : begin + TABLE]

        def span(which):
            return (0, T_ROWS, TOP_ROWS) if which is ta else (1, SIDE, 0)

        def multiply_words(n, which, iwh):
            first, last, window_row = span(which)
            multiply_rows(which[(n, iwh)], n, iwh, first, last, window_row - first)

        second_held = keep.tile([P, SIDE, LOWER], BF16)
        lower_wins = keep.tile([P, WIN_ROWS, LOWER], BF16)

        def derive(n):
            lower = wins[n][:].bitcast(F32)[:, :, 0 : ROW // 2 : 2]
            nc.scalar.copy(
                out=lower_wins[:].bitcast(F32).rearrange("p u (w g) -> p u w g", g=2),
                in_=lower.rearrange("p u (g w) -> p u w g", g=2)[:, :, :, ::-1],
            )
            first_words = held_rows(n, 0).bitcast(F32)
            second_words = second_held[:].bitcast(F32)
            nc.scalar.copy(
                out=second_words[:, :, 0 : GRID - 2].rearrange("p u (w g) -> p u w g", g=2),
                in_=first_words[:, :, 1 : GRID - 1].rearrange("p u (g w) -> p u w g", g=2),
            )
            nc.scalar.copy(out=second_words[:, :, GRID - 1 : GRID], in_=first_words[:, :, GRID - 1 : GRID])
            beyond = held_tile(n)[:, HELD:].bitcast(F32).rearrange("p (u f) -> p u f", f=2)
            nc.scalar.copy(out=second_words[:, :, GROUP - 2 : GRID : GROUP], in_=beyond)

        def multiply_lower(n, which):
            first, last, begin = span(which)
            end = begin + last - first
            nc.vector.tensor_tensor(
                out=which[(n, 1)].rearrange("p (u e) -> p u e", e=ROW)[:, first:last, LOWER:ROW],
                in0=second_held[:, first:last, :],
                in1=lower_wins[:, begin:end, :],
                op=mybir.AluOpType.mult,
            )
            words = wins[n][:, begin:end, :].rearrange("p u (f q r t) -> p u f q r t", f=PHASES, q=QUADS, r=2)
            edges = stores[(n, "ta" if which is ta else "tb")][:, EDGES:STORE]
            nc.vector.tensor_tensor(
                out=edges.rearrange("p (u f t) -> p u f t", f=2, t=PAIR)[:, first:last],
                in0=second_held[:, first:last, :].rearrange("p u (f q g t) -> p u f q g t", f=2, q=QUADS, g=2)[
                    :, :, :, QUADS - 1, 0, :
                ],
                in1=words[:, :, 2:PHASES, QUADS - 1, 1, :],
                op=mybir.AluOpType.mult,
            )

        def compose(n, which):
            first, last, begin = span(which)
            row = ROW // 2
            words = stores[(n, "ta" if which is ta else "tb")][:].bitcast(F32)
            out_rows = words[:, 0 : TABLE // 2].rearrange("p (u e) -> p u e", e=row)[:, first:last]
            for group in range(2):
                lower = row * first + row // 2 + (1 - group)
                step = FIRST // 2 + row * first + (GRID if group == 0 else PAIR) - lower
                two = words[:, 0 : 2 * step].rearrange("p (r s) -> p r s", r=2)
                source = two[:, :, lower : lower + row * (last - first)].rearrange("p r (u e) -> p u e r", e=row)
                nc.scalar.copy(
                    out=out_rows[:, :, GRID * group : GRID * (group + 1)].rearrange("p u (w r) -> p u w r", r=2),
                    in_=source[:, :, 0:GRID:2, :],
                )
            edges = words[:, EDGES // 2 : STORE // 2].rearrange("p (u f) -> p u f", f=2)
            nc.scalar.copy(out=out_rows[:, :, 3 * GRID // 2 - 1 :: GRID // 2], in_=edges[:, first:last])

        def spread(n, which, iwh):
            first = 0 if which is ta else 1
            rows = slice(ROW * first, ROW * (first + T_ROWS))
            nc.sync.dma_start(out=which[(SPREAD, iwh)][n + 1 : P : SLOTS, rows], in_=which[(n, iwh)][0:P:SLOTS, rows])

        def place_squares(n, which, iwh):
            nc.sync.dma_start(out=which[(n, iwh)][0:P:SLOTS], in_=squares[iwh][n:P:SLOTS])

        def exchange(n, ih, iwh):
            target, source, slot = (ta, tb, 3) if ih == 1 else (tb, ta, 1)
            rows = slice(ROW * ih, ROW * (ih + GRID))
            nc.sync.dma_start(out=target[(n, iwh)][slot:P:SLOTS, rows], in_=source[(n, iwh)][slot:P:SLOTS, rows])

        sums = {}
        results = {}
        done = {}

        def warm_tensor(n, table):
            sums[(n, 0, 0)] = psum.tile([P, N_TILE], F32, name="sums00")
            done[(n, 0, 0)] = 0
            for repeat in range(WARM_UPS):
                nc.tensor.matmul(
                    out=sums[(n, 0, 0)][:], lhsT=table[:, 0:P], rhs=table[:, 0:N_TILE], start=True, stop=True
                )

        def contract(n, ih, iwh, halves):
            a = 2 * ih + iwh
            width = len(halves) * N_TILE
            table = (ta if ih < 2 else tb)[(n, iwh)]
            codes = packed.tile([P, HALVES * N_TILE], U32, name="codes", align_bytes=64)
            scales = packed.tile([P, HALVES * N_TILE], U8, name="scales", align_bytes=64)
            begin = ROW * ih + PACK * N_TILE * halves[0]
            nc.vector.quantize_mx(
                out=codes[:, 0:width].bitcast(FP8X4), scales=scales[:, 0:width], in_=table[:, begin : begin + PACK * width]
            )
            for place, half in enumerate(halves):
                for m in range(M_TILES):
                    if (n, half, m) not in sums:
                        sums[(n, half, m)] = psum.tile([P, N_TILE], F32, name="sums%d%d" % (half, m))
                        done[(n, half, m)] = 0
                    nc.tensor.matmul_mx(
                        out=sums[(n, half, m)][:],
                        lhsT=w_words[ih][:, iwh, 2 * P * m : 2 * P * (m + 1)].bitcast(FP4X4),
                        lhsT_scale=w_planes[:, a, P * m : P * (m + 1)],
                        rhs=codes[:, N_TILE * place : N_TILE * (place + 1)].bitcast(FP8X4),
                        rhs_scale=scales[:, N_TILE * place : N_TILE * (place + 1)],
                        start=(done[(n, half, m)] == 0),
                        stop=(done[(n, half, m)] == PASSES - 1),
                    )
                    done[(n, half, m)] += 1

        def empty(n, half):
            results[(n, half)] = outs.tile([P, M_TILES, TILE_ROWS, QUADS, PHASES], F32, name="result")
            for m in range(M_TILES):
                nc.scalar.copy(out=results[(n, half)][:, m], in_=bank_rows(n, half, m))

        def bank_rows(n, half, m):
            return sums[(n, half, m)][:].rearrange("o (y s q) -> o y q s", s=PHASES, y=TILE_ROWS)

        def store(n, half):
            rows = out[n, :, TILE_ROWS * half : TILE_ROWS * (half + 1), :].rearrange("(m o) y z -> o m (y z)", m=M_TILES)
            nc.sync.dma_start(out=rows, in_=results[(n, half)][:].rearrange("o m y q s -> o m (y q s)"))

        def finish(half, copies):
            result = outs.tile([P, M_TILES, TILE_ROWS, QUADS, PHASES], F32, name="result")
            for m in range(M_TILES):
                copies[m](out=result[:, m], in_=bank_rows(SPREAD, half, m))
            for m in range(M_TILES):
                nc.sync.dma_start(
                    out=out[SPREAD, P * m : P * (m + 1), TILE_ROWS * half : TILE_ROWS * (half + 1), :].rearrange(
                        "o y z -> o (y z)"
                    ),
                    in_=result[:, m].rearrange("o y q s -> o (y q s)"),
                )

        both = list(range(HALVES))

        def pass_of(n, ih):
            for iwh in range(2):
                contract(n, ih, iwh, both)

        def inner_passes(n):
            pass_of(n, 1)
            pass_of(n, 2)
            for half in both:
                empty(n, half)

        image_rows = x_rows[:].rearrange("p (r w) -> p r w", w=SIDE)
        for phase in range(PHASES):
            columns = slice(GRID * phase, GRID * (phase + 1))
            nc.vector.tensor_copy(out=wins[SQUARES][:, :, columns], in_=image_rows[:, :, phase : phase + GRID])
        fill_windows(0)
        turn_words(3)

        def copy_held(k, iwh, phase):
            first, last = BANKS[k]
            rows = banks[k][:, 0 : (last - first) * SIDE].rearrange("p (h w) -> p h w", w=SIDE)
            shift = 2 * iwh + phase
            every_fourth = rows[:, :, shift : shift + PACK * (QUADS - 1) + 1 : PACK]
            target = held_rows(SQUARES, iwh)[:, first:last, :].rearrange("p u (f q t) -> p u f q t", f=PHASES, q=QUADS)
            nc.scalar.copy(
                out=target[:, :, phase], in_=every_fourth.unsqueeze(3).to_broadcast([P, last - first, QUADS, PAIR])
            )

        for k, (first, last) in enumerate(BANKS):
            for phase in range(PHASES):
                copy_held(k, 0, phase)
            multiply_rows(squares[0], SQUARES, 0, first, last, 0)
        beyond = held_tile(SQUARES)[:, HELD:].rearrange("p (u f t) -> p u f t", f=2, t=PAIR)
        for k, (first, last) in enumerate(BANKS):
            rows = banks[k][:, 0 : (last - first) * SIDE].rearrange("p (h w) -> p h w", w=SIDE)
            nc.scalar.copy(
                out=beyond[:, first:last],
                in_=rows[:, :, GRID : GRID + 2].unsqueeze(3).to_broadcast([P, last - first, 2, PAIR]),
            )
        fill_held(0)
        nc.vector.tensor_copy(
            out=held_rows(SQUARES, 1)[:, :, 0 : LOWER // 2], in_=held_rows(SQUARES, 0)[:, :, LOWER // 2 :]
        )
        for k, (first, last) in enumerate(BANKS):
            for phase in range(2, PHASES):
                copy_held(k, 1, phase)
            multiply_rows(squares[1], SQUARES, 1, first, last, 0)
        derive(0)
        fill_windows(1)
        fill_held(1)
        for ih in (1, 2):
            turn_words(ih)

        def streams(n, which):
            open_store(n, which)
            multiply_words(n, which, 0)
            multiply_lower(n, which)
            compose(n, which)

        def spread_both(n, which):
            for iwh in range(2):
                spread(n, which, iwh)

        def place_both(n, which):
            for iwh in range(2):
                place_squares(n, which, iwh)

        def exchange_both(n, ih):
            for iwh in range(2):
                exchange(n, ih, iwh)

        streams(0, ta)
        streams(0, tb)
        derive(1)
        spread_both(0, ta)
        fill_held(2)
        place_both(0, ta)
        spread_both(0, tb)
        place_both(0, tb)
        for which in (ta, tb):
            open_store(1, which)
            multiply_words(1, which, 0)
        warm_tensor(0, tb[(1, 0)][:, ROW:])
        pass_of(0, 0)
        exchange_both(0, 1)
        fill_windows(2)
        multiply_lower(1, ta)
        compose(1, ta)
        pass_of(0, 3)
        exchange_both(0, 2)
        spread_both(1, ta)
        multiply_lower(1, tb)
        compose(1, tb)
        derive(2)
        spread_both(1, tb)
        place_both(1, ta)
        inner_passes(0)
        place_both(1, tb)
        for which in (ta, tb):
            place_both(SPREAD, which)
        streams(2, ta)
        warm_tensor(1, ta[(2, 0)])
        for half in both:
            store(0, half)
        pass_of(1, 0)
        exchange_both(1, 1)
        spread_both(2, ta)
        pass_of(1, 3)
        exchange_both(1, 2)
        place_both(2, ta)
        streams(2, tb)
        warm_tensor(2, tb[(2, 0)][:, ROW:])
        inner_passes(1)
        spread_both(2, tb)
        place_both(2, tb)
        pass_of(2, 0)
        exchange_both(2, 1)
        pass_of(SPREAD, 0)
        exchange_both(SPREAD, 1)
        pass_of(2, 3)
        exchange_both(2, 2)
        for half in both:
            store(1, half)
        pass_of(SPREAD, 3)
        exchange_both(SPREAD, 2)
        inner_passes(2)
        for half in both:
            store(2, half)

        for iwh in range(2):
            contract(SPREAD, 1, iwh, both)
        contract(SPREAD, 2, 0, both)
        contract(SPREAD, 2, 1, [0])
        finish(0, [nc.scalar.copy, nc.scalar.copy])
        contract(SPREAD, 2, 1, [1])
        finish(1, [nc.scalar.copy, nc.vector.tensor_copy])
